import numpy as np
import ml_dtypes


def mxq(x, axis, fmt="e4m3"):
    dtype, down = {"e4m3": (ml_dtypes.float8_e4m3fn, 7), "e5m2": (ml_dtypes.float8_e5m2, 14)}[fmt]
    v = np.moveaxis(np.asarray(x, np.float32).astype(ml_dtypes.bfloat16).astype(np.float64), axis, -1)
    blocks = v.reshape(v.shape[:-1] + (-1, 32))
    amax = np.abs(blocks).max(-1, keepdims=True)
    byte = np.maximum(np.where(amax > 0, np.frexp(amax)[1] - 1 + 127, 0) - down, 1)
    scale = np.exp2(byte - 127.0)
    codes = (blocks / scale).astype(np.float32).astype(dtype).astype(np.float64)
    return np.moveaxis((codes * scale).reshape(v.shape), -1, axis)


WIDE = False


def mx_kscale(k):
    if not WIDE:
        return np.ones(k)
    levels = np.array([10, -10, 5, -5, 0])
    a = np.random.permutation(np.resize(levels, k // 512 * 4)).reshape(k // 512, 4)
    idx = np.arange(k)
    return np.exp2(a[idx // 512, idx % 128 // 32])


BF16 = ml_dtypes.bfloat16


def bf(x):
    return np.asarray(x, np.float32).astype(BF16)


def f64(x):
    return np.asarray(x).astype(np.float64)


E2M1 = np.array([0.0, 0.5, 1.0, 1.5, 2.0, 3.0, 4.0, 6.0, -0.0, -0.5, -1.0, -1.5, -2.0, -3.0, -4.0, -6.0])


def pack_weight(w, fmt):
    k, n = w.shape
    w = f64(bf(w)).reshape(k // 32, 32, n)
    amax = np.abs(w).max(1)
    if fmt == "e4m3":
        byte = np.frexp(amax)[1] - 1 + 127 - 7
    else:
        mant, ex = np.frexp(amax / 6.0)
        byte = np.where(mant > 0.5, ex, ex - 1) + 127
    byte = np.clip(np.where(amax > 0, byte, 1), 1, 254)
    scaled = (w * np.exp2(127.0 - byte)[:, None, :]).reshape(k, n).astype(np.float32)
    by_word = np.ascontiguousarray(scaled.reshape(k // 512, 128, 4, n).transpose(0, 1, 3, 2))
    if fmt == "e4m3":
        words = by_word.astype(ml_dtypes.float8_e4m3fn).view(np.uint8)
    else:
        c = by_word.astype(ml_dtypes.float4_e2m1fn).view(np.uint8) & 0xF
        words = c[..., 0::2] | (c[..., 1::2] << 4)
    return np.ascontiguousarray(words), np.ascontiguousarray(byte.astype(np.uint8).reshape(k // 512, 16, n))


def unpack_weight(words, scales, fmt):
    g, p, n, _ = words.shape
    if fmt == "e4m3":
        vals = np.ascontiguousarray(words).view(ml_dtypes.float8_e4m3fn).astype(np.float64)
    else:
        nib = np.empty((g, p, n, 4), np.uint8)
        nib[..., 0::2] = words & 0xF
        nib[..., 1::2] = words >> 4
        vals = E2M1[nib]
    vals = vals * np.repeat(np.exp2(scales.astype(np.float64) - 127.0), 8, axis=1)[..., None]
    return vals.transpose(0, 1, 3, 2).reshape(g * 512, n)

def pack4(w):
    words, scales = pack_weight(w, "e2m1")
    return words.reshape(words.shape[0], 128, -1), scales


def unpack4(words, scales):
    return unpack_weight(words.reshape(words.shape[0], 128, -1, 2), scales, "e2m1")


B, L, C, H, BLK = 8, 512, 512, 8, 128
D = C // H
MAX_SCALE_MUL = np.log(100.0)
EPS = 1e-12


def l2norm(t):
    n = np.sqrt(np.sum(t * t, axis=-1, keepdims=True))
    return t / np.maximum(n, EPS)


def setup_inputs():
    s = mx_kscale(C)
    lsm = np.linspace(np.log(4.0), MAX_SCALE_MUL + 1.0, H) + 0.05 * np.random.standard_normal(H)
    x = bf(np.random.standard_normal((B, L, C)) * s)
    w = np.random.standard_normal((3 * C, C)) / np.sqrt(C) / s[None, :]
    words, scales = pack4(np.ascontiguousarray(w.T))
    q_bias = bf(np.random.standard_normal(C) * 0.3)
    v_bias = bf(np.random.standard_normal(C) * 0.3)
    return {"x": x,
            "W_qkv_words": words,
            "W_qkv_scales": scales,
            "q_bias": q_bias,
            "v_bias": v_bias,
            "log_scale_mul": bf(lsm.reshape(1, H, 1, 1))}


def reference(x, W_qkv_words, W_qkv_scales, q_bias, v_bias, log_scale_mul):
    qb = f64(q_bias)
    bias = np.concatenate([qb, np.zeros_like(qb), f64(v_bias)])
    qkv = (mxq(f64(x), 2, "e4m3") @ unpack4(W_qkv_words, W_qkv_scales)) + bias
    qkv = qkv.reshape(B, L, 3, H, D)
    q, k, v = np.moveaxis(qkv, 2, 0)
    q = np.swapaxes(q, 1, 2)
    k = np.swapaxes(k, 1, 2)
    v = np.swapaxes(v, 1, 2)
    scale_mul = np.exp(np.minimum(f64(log_scale_mul), MAX_SCALE_MUL))
    q = l2norm(q) * scale_mul
    k = l2norm(k)
    return q, k, v

@@ -1,0 +1,213 @@
+import math
+from contextlib import ExitStack
+
+import concourse.mybir as mybir
+from concourse.masks import make_identity
+
+F32 = mybir.dt.float32
+BF16 = mybir.dt.bfloat16
+I32 = mybir.dt.int32
+U32 = mybir.dt.uint32
+U8 = mybir.dt.uint8
+FP8X4 = mybir.dt.float8_e4m3fn_x4
+FP4X4 = mybir.dt.float4_e2m1fn_x4
+ALU = mybir.AluOpType
+ACT = mybir.ActivationFunctionType
+
+B, L, C, H, D = 8, 512, 512, 8, 64
+P = 128
+J = L // P
+PACK = 4
+Q, K, V = 0, 1, 2
+EPS = 1e-12
+MAX_LOG_GAIN = math.log(100.0)
+FLOPS = 2 * B * L * C * 3 * C
+
+
+def tile_selfattention_pa_t_kernel(
+    tc, x, W_qkv_words, W_qkv_scales, q_bias, v_bias, log_scale_mul, out_0, out_1, out_2
+):
+    nc = tc.nc
+    with ExitStack() as ctx:
+        ctx.enter_context(tc.manual_schedule())
+        consts = ctx.enter_context(tc.tile_pool(name="consts", bufs=1))
+        stage = ctx.enter_context(tc.tile_pool(name="stage", bufs=2))
+        results = ctx.enter_context(tc.tile_pool(name="results", bufs=3))
+        psum_k = ctx.enter_context(tc.psum_pool(name="psum_k", bufs=J))
+        psum_ring = ctx.enter_context(tc.psum_pool(name="psum_ring", bufs=4))
+
+        w_scales = consts.tile([P, 3 * C], U8, align_bytes=64)
+        nc.vector.memset(w_scales[:].bitcast(I32), 0)
+        for quadrant in range(4):
+            nc.sync.dma_start(
+                out=w_scales[32 * quadrant : 32 * quadrant + 4, :].bitcast(I32),
+                in_=W_qkv_scales[0, 4 * quadrant : 4 * quadrant + 4, :].bitcast(I32),
+            )
+        x_sb = [consts.tile([P, J, C], BF16, name="x_sb%d" % b) for b in range(B)]
+
+        def load_x(b):
+            nc.sync.dma_start(out=x_sb[b][:], in_=x[b].rearrange("(p j) c -> p j c", j=J))
+
+        load_x(0)
+        w_words = consts.tile([P, 2 * 3 * C], U8, align_bytes=64)
+        nc.sync.dma_start(out=w_words[:].bitcast(I32), in_=W_qkv_words[0].bitcast(I32))
+        log_gain = consts.tile([P, H], BF16)
+        nc.sync.dma_start(
+            out=log_gain[:], in_=log_scale_mul.rearrange("a h b c -> (a h b c)").partition_broadcast(P)
+        )
+        q_bias_sb = consts.tile([P, H, D], BF16)
+        nc.sync.dma_start(out=q_bias_sb[:].rearrange("p h d -> p (h d)"), in_=q_bias.partition_broadcast(P))
+        v_bias_sb = consts.tile([P, H, D], BF16)
+        nc.sync.dma_start(out=v_bias_sb[:].rearrange("p h d -> p (h d)"), in_=v_bias.partition_broadcast(P))
+        for b in range(1, B):
+            load_x(b)
+
+        identity = consts.tile([P, P], F32)
+        make_identity(nc, identity[:])
+
+        log_clamped = consts.tile([P, H], F32)
+        nc.vector.tensor_scalar_min(out=log_clamped[:], in0=log_gain[:], scalar1=MAX_LOG_GAIN)
+        inv_gain_sq = consts.tile([P, H], F32)
+        nc.scalar.activation(out=inv_gain_sq[:], in_=log_clamped[:], func=ACT.Exp, scale=-2.0)
+        table_warm = consts.tile([P, H], F32)
+        nc.scalar.activation(out=table_warm[:], in_=inv_gain_sq[:], func=ACT.Abs_reciprocal_sqrt)
+
+        def transpose_words(b):
+            banks = []
+            for half in range(2):
+                bank = psum_ring.tile([P, 2, 2, P], F32, tag="ring")
+                for jj in range(2):
+                    words = x_sb[b][:, 2 * half + jj, :].bitcast(F32)
+                    for u in range(2):
+                        nc.tensor.transpose(bank[:, jj, u, :], words[:, u : C // 2 : 2], identity[:])
+                banks.append(bank)
+            return banks
+
+        def regroup(banks):
+            grouped = stage.tile([P, J, P, PACK], BF16, align_bytes=64, tag="grouped")
+            for half in range(2):
+                nc.vector.tensor_copy(
+                    out=grouped[:, 2 * half : 2 * half + 2]
+                    .rearrange("p j r t -> p (j r t)")
+                    .bitcast(F32)
+                    .rearrange("p (j r u) -> p j r u", j=2, u=2),
+                    in_=banks[half][:].rearrange("p j u r -> p j r u"),
+                )
+            return grouped
+
+        def quantise(grouped):
+            codes = stage.tile([P, J * P], U32, align_bytes=64, tag="codes")
+            scales = stage.tile([P, J * P], U8, align_bytes=64, tag="scales")
+            nc.vector.quantize_mx(
+                out=codes[:].bitcast(FP8X4),
+                scales=scales[:],
+                in_=grouped[:].rearrange("p j r t -> p (j r t)"),
+            )
+            return codes, scales
+
+        def project(block, x_mx, j, pool, tag):
+            codes, scales = x_mx
+            acc = pool.tile([P, H, D], F32, tag=tag)
+            nc.tensor.matmul_mx(
+                out=acc[:].rearrange("p h d -> p (h d)"),
+                lhsT=codes[:, j * P : (j + 1) * P].bitcast(FP8X4),
+                lhsT_scale=scales[:, j * P : (j + 1) * P],
+                rhs=w_words[:, block * 2 * C : (block + 1) * 2 * C].bitcast(FP4X4),
+                rhs_scale=w_scales[:, block * C : (block + 1) * C],
+                start=True,
+                stop=True,
+            )
+            return acc
+
+        def project_and_add_bias(block, x_mx, j, bias, res):
+            acc = project(block, x_mx, j, psum_ring, "ring")
+            nc.vector.tensor_tensor(out=res[:, :, j, :], in0=acc[:], in1=bias[:], op=ALU.add)
+
+        def sum_squares(rows, squares, sums, j):
+            for h in range(H):
+                nc.scalar.activation(
+                    out=squares[:, h, j, :], in_=rows[:, h, :], func=ACT.Square, accum_out=sums[:, h, j : j + 1]
+                )
+
+        def store(dst, b, heads, res):
+            nc.sync.dma_start(
+                out=dst[b, heads].rearrange("h (p j) d -> p h (j d)", j=J),
+                in_=res[:, heads].rearrange("p h j d -> p h (j d)"),
+            )
+
+        def finish_q(b, q_res, q_scaled, second_engine):
+            q_factor = stage.tile([P, H, J], F32, tag="q_factor")
+            nc.scalar.activation(out=q_factor[:], in_=q_scaled[:], func=ACT.Abs_reciprocal_sqrt)
+            for engine, first_head in ((nc.gpsimd, 0), (second_engine, H // 2)):
+                heads = slice(first_head, first_head + H // 2)
+                rows = q_res[:, heads].rearrange("p h j d -> p (h j) d")
+                factor = q_factor[:, heads].rearrange("p h j -> p (h j)").unsqueeze(2)
+                engine.tensor_tensor(out=rows, in0=rows, in1=factor.to_broadcast([P, H // 2 * J, D]), op=ALU.mult)
+                store(out_0, b, heads, q_res)
+
+        all_heads = slice(0, H)
+        x_mx = quantise(regroup(transpose_words(0)))
+        banks = transpose_words(1)
+        k_acc = [project(K, x_mx, j, psum_k, "k") for j in range(J)]
+        x_mx_next = None
+        q_res = None
+        q_scaled = None
+
+        for b in range(B):
+            k_sums = stage.tile([P, H, J], F32, tag="k_sums")
+            k_squares = stage.tile([P, H, J, D], BF16, tag="k_squares")
+            sum_squares(k_acc[0], k_squares, k_sums, 0)
+            if b > 0:
+                finish_q(b - 1, q_res, q_scaled, nc.gpsimd)
+            for j in range(1, J):
+                sum_squares(k_acc[j], k_squares, k_sums, j)
+
+            if b + 1 < B:
+                grouped = regroup(banks)
+            q_res = results.tile([P, H, J, D], F32, tag="q")
+            for j in range(J):
+                project_and_add_bias(Q, x_mx, j, q_bias_sb, q_res)
+            if b + 1 < B:
+                x_mx_next = quantise(grouped)
+
+            q_sums = stage.tile([P, H, J], F32, tag="q_sums")
+            q_squares = stage.tile([P, H, J, D], BF16, tag="q_squares")
+            sum_squares(q_res[:, :, 0, :], q_squares, q_sums, 0)
+            k_clamped = stage.tile([P, H, J], F32, tag="k_clamped")
+            nc.vector.tensor_scalar_max(out=k_clamped[:], in0=k_sums[:], scalar1=EPS * EPS)
+            k_factor = stage.tile([P, H, J], F32, tag="k_factor")
+            nc.scalar.activation(out=k_factor[:], in_=k_clamped[:], func=ACT.Abs_reciprocal_sqrt)
+            for j in range(1, J):
+                sum_squares(q_res[:, :, j, :], q_squares, q_sums, j)
+
+            v_res = results.tile([P, H, J, D], F32, tag="v")
+            for j in range(J):
+                project_and_add_bias(V, x_mx, j, v_bias_sb, v_res)
+            store(out_2, b, all_heads, v_res)
+            if b + 2 < B:
+                banks = transpose_words(b + 2)
+
+            k_res = results.tile([P, H, J, D], F32, tag="k")
+            for j in range(J):
+                nc.vector.tensor_tensor(
+                    out=k_res[:, :, j, :],
+                    in0=k_acc[j][:],
+                    in1=k_factor[:, :, j : j + 1].to_broadcast([P, H, D]),
+                    op=ALU.mult,
+                )
+                if b + 1 < B:
+                    k_acc[j] = project(K, x_mx_next, j, psum_k, "k")
+            store(out_1, b, all_heads, k_res)
+
+            q_scaled = stage.tile([P, H, J], F32, tag="q_scaled")
+            nc.vector.scalar_tensor_tensor(
+                out=q_scaled[:],
+                in0=q_sums[:],
+                scalar=EPS * EPS,
+                in1=inv_gain_sq[:].unsqueeze(2).to_broadcast([P, H, J]),
+                op0=ALU.max,
+                op1=ALU.mult,
+            )
+            x_mx = x_mx_next
+
+        finish_q(B - 1, q_res, q_scaled, nc.vector)

@@ -86,7 +86,7 @@ def tile_selfattention_pa_t_kernel(
         def regroup(banks):
             grouped = stage.tile([P, J, P, PACK], BF16, align_bytes=64, tag="grouped")
             for half in range(2):
-                nc.vector.tensor_copy(
+                nc.scalar.copy(
                     out=grouped[:, 2 * half : 2 * half + 2]
                     .rearrange("p j r t -> p (j r t)")
                     .bitcast(F32)
@@ -154,6 +154,9 @@ def tile_selfattention_pa_t_kernel(
         q_scaled = None
 
         for b in range(B):
+            if b + 1 < B:
+                grouped = regroup(banks)
+
             k_sums = stage.tile([P, H, J], F32, tag="k_sums")
             k_squares = stage.tile([P, H, J, D], BF16, tag="k_squares")
             sum_squares(k_acc[0], k_squares, k_sums, 0)
@@ -162,8 +165,6 @@ def tile_selfattention_pa_t_kernel(
             for j in range(1, J):
                 sum_squares(k_acc[j], k_squares, k_sums, j)
 
-            if b + 1 < B:
-                grouped = regroup(banks)
             q_res = results.tile([P, H, J, D], F32, tag="q")
             for j in range(J):
                 project_and_add_bias(Q, x_mx, j, q_bias_sb, q_res)

@@ -86,7 +86,7 @@ def tile_selfattention_pa_t_kernel(
         def regroup(banks):
             grouped = stage.tile([P, J, P, PACK], BF16, align_bytes=64, tag="grouped")
             for half in range(2):
-                nc.scalar.copy(
+                nc.vector.tensor_copy(
                     out=grouped[:, 2 * half : 2 * half + 2]
                     .rearrange("p j r t -> p (j r t)")
                     .bitcast(F32)
@@ -129,6 +129,8 @@ def tile_selfattention_pa_t_kernel(
                     out=squares[:, h, j, :], in_=rows[:, h, :], func=ACT.Square, accum_out=sums[:, h, j : j + 1]
                 )
 
+        head_halves = (slice(0, H // 2), slice(H // 2, H))
+
         def store(dst, b, heads, res):
             nc.sync.dma_start(
                 out=dst[b, heads].rearrange("h (p j) d -> p h (j d)", j=J),
@@ -138,14 +140,12 @@ def tile_selfattention_pa_t_kernel(
         def finish_q(b, q_res, q_scaled, second_engine):
             q_factor = stage.tile([P, H, J], F32, tag="q_factor")
             nc.scalar.activation(out=q_factor[:], in_=q_scaled[:], func=ACT.Abs_reciprocal_sqrt)
-            for engine, first_head in ((nc.gpsimd, 0), (second_engine, H // 2)):
-                heads = slice(first_head, first_head + H // 2)
+            for engine, heads in zip((nc.gpsimd, second_engine), head_halves):
                 rows = q_res[:, heads].rearrange("p h j d -> p (h j) d")
                 factor = q_factor[:, heads].rearrange("p h j -> p (h j)").unsqueeze(2)
                 engine.tensor_tensor(out=rows, in0=rows, in1=factor.to_broadcast([P, H // 2 * J, D]), op=ALU.mult)
                 store(out_0, b, heads, q_res)
 
-        all_heads = slice(0, H)
         x_mx = quantise(regroup(transpose_words(0)))
         banks = transpose_words(1)
         k_acc = [project(K, x_mx, j, psum_k, "k") for j in range(J)]
@@ -154,9 +154,6 @@ def tile_selfattention_pa_t_kernel(
         q_scaled = None
 
         for b in range(B):
-            if b + 1 < B:
-                grouped = regroup(banks)
-
             k_sums = stage.tile([P, H, J], F32, tag="k_sums")
             k_squares = stage.tile([P, H, J, D], BF16, tag="k_squares")
             sum_squares(k_acc[0], k_squares, k_sums, 0)
@@ -165,6 +162,8 @@ def tile_selfattention_pa_t_kernel(
             for j in range(1, J):
                 sum_squares(k_acc[j], k_squares, k_sums, j)
 
+            if b + 1 < B:
+                grouped = regroup(banks)
             q_res = results.tile([P, H, J, D], F32, tag="q")
             for j in range(J):
                 project_and_add_bias(Q, x_mx, j, q_bias_sb, q_res)
@@ -184,7 +183,8 @@ def tile_selfattention_pa_t_kernel(
             v_res = results.tile([P, H, J, D], F32, tag="v")
             for j in range(J):
                 project_and_add_bias(V, x_mx, j, v_bias_sb, v_res)
-            store(out_2, b, all_heads, v_res)
+            for heads in head_halves:
+                store(out_2, b, heads, v_res)
             if b + 2 < B:
                 banks = transpose_words(b + 2)
 
@@ -198,7 +198,8 @@ def tile_selfattention_pa_t_kernel(
                 )
                 if b + 1 < B:
                     k_acc[j] = project(K, x_mx_next, j, psum_k, "k")
-            store(out_1, b, all_heads, k_res)
+            for heads in head_halves:
+                store(out_1, b, heads, k_res)
 
             q_scaled = stage.tile([P, H, J], F32, tag="q_scaled")
             nc.vector.scalar_tensor_tensor(

@@ -16,9 +16,17 @@ ACT = mybir.ActivationFunctionType
 
 B, L, C, H, D = 8, 512, 512, 8, 64
 P = 128
-J = L // P
 PACK = 4
+E = 2
+J = E * L // P
+CHUNK = 4
+CHUNKS = B * L // (P * CHUNK)
+HR = 4
+ROUNDS = (B // E) * (H // HR)
+PAIR = 2
+BANKS = J // PAIR
 Q, K, V = 0, 1, 2
+GAIN_ROW, V_ROW, Q_ROW = 0, 1, 2
 EPS = 1e-12
 MAX_LOG_GAIN = math.log(100.0)
 FLOPS = 2 * B * L * C * 3 * C
@@ -32,10 +40,23 @@ def tile_selfattention_pa_t_kernel(
         ctx.enter_context(tc.manual_schedule())
         consts = ctx.enter_context(tc.tile_pool(name="consts", bufs=1))
         stage = ctx.enter_context(tc.tile_pool(name="stage", bufs=2))
-        results = ctx.enter_context(tc.tile_pool(name="results", bufs=3))
-        psum_k = ctx.enter_context(tc.psum_pool(name="psum_k", bufs=J))
+        results = ctx.enter_context(tc.tile_pool(name="results", bufs=4))
+        psum_k = ctx.enter_context(tc.psum_pool(name="psum_k", bufs=BANKS))
         psum_ring = ctx.enter_context(tc.psum_pool(name="psum_ring", bufs=4))
 
+        x_sb = [consts.tile([P, CHUNK, C], BF16, name="x_sb%d" % c) for c in range(CHUNKS)]
+
+        def load_x(c):
+            group, j0 = c // 2, CHUNK * (c % 2)
+            tokens = x[E * group : E * group + E].rearrange("e (s j) c -> s e j c", j=J)
+            nc.sync.dma_start(out=x_sb[c][:], in_=tokens[:, :, j0 : j0 + CHUNK, :])
+
+        load_x(0)
+        small_rows = consts.tile([P, 3, C], BF16)
+        nc.vector.memset(small_rows[:].rearrange("p r c -> p (r c)").bitcast(I32), 0)
+        nc.sync.dma_start(out=small_rows[0:1, GAIN_ROW, 0:H], in_=log_scale_mul.rearrange("a h b c -> (a b c) h"))
+        nc.sync.dma_start(out=small_rows[0:1, V_ROW, :], in_=v_bias.unsqueeze(0))
+        nc.sync.dma_start(out=small_rows[0:1, Q_ROW, :], in_=q_bias.unsqueeze(0))
         w_scales = consts.tile([P, 3 * C], U8, align_bytes=64)
         nc.vector.memset(w_scales[:].bitcast(I32), 0)
         for quadrant in range(4):
@@ -43,173 +64,200 @@ def tile_selfattention_pa_t_kernel(
                 out=w_scales[32 * quadrant : 32 * quadrant + 4, :].bitcast(I32),
                 in_=W_qkv_scales[0, 4 * quadrant : 4 * quadrant + 4, :].bitcast(I32),
             )
-        x_sb = [consts.tile([P, J, C], BF16, name="x_sb%d" % b) for b in range(B)]
-
-        def load_x(b):
-            nc.sync.dma_start(out=x_sb[b][:], in_=x[b].rearrange("(p j) c -> p j c", j=J))
-
-        load_x(0)
         w_words = consts.tile([P, 2 * 3 * C], U8, align_bytes=64)
         nc.sync.dma_start(out=w_words[:].bitcast(I32), in_=W_qkv_words[0].bitcast(I32))
-        log_gain = consts.tile([P, H], BF16)
-        nc.sync.dma_start(
-            out=log_gain[:], in_=log_scale_mul.rearrange("a h b c -> (a h b c)").partition_broadcast(P)
-        )
-        q_bias_sb = consts.tile([P, H, D], BF16)
-        nc.sync.dma_start(out=q_bias_sb[:].rearrange("p h d -> p (h d)"), in_=q_bias.partition_broadcast(P))
-        v_bias_sb = consts.tile([P, H, D], BF16)
-        nc.sync.dma_start(out=v_bias_sb[:].rearrange("p h d -> p (h d)"), in_=v_bias.partition_broadcast(P))
-        for b in range(1, B):
-            load_x(b)
+        for c in range(1, CHUNKS):
+            load_x(c)
 
         identity = consts.tile([P, P], F32)
         make_identity(nc, identity[:])
 
-        log_clamped = consts.tile([P, H], F32)
-        nc.vector.tensor_scalar_min(out=log_clamped[:], in0=log_gain[:], scalar1=MAX_LOG_GAIN)
-        inv_gain_sq = consts.tile([P, H], F32)
-        nc.scalar.activation(out=inv_gain_sq[:], in_=log_clamped[:], func=ACT.Exp, scale=-2.0)
-        table_warm = consts.tile([P, H], F32)
-        nc.scalar.activation(out=table_warm[:], in_=inv_gain_sq[:], func=ACT.Abs_reciprocal_sqrt)
+        ones = consts.tile([P, P], BF16)
+        nc.vector.memset(ones[:], 1.0)
 
-        def transpose_words(b):
+        def spread(row, width):
+            bank = psum_ring.tile([P, C], F32, tag="ring")
+            nc.tensor.matmul(out=bank[:, 0:width], lhsT=ones[:], rhs=small_rows[:, row, 0:width], start=True, stop=True)
+            return bank
+
+        def transpose_words(c):
             banks = []
-            for half in range(2):
-                bank = psum_ring.tile([P, 2, 2, P], F32, tag="ring")
-                for jj in range(2):
-                    words = x_sb[b][:, 2 * half + jj, :].bitcast(F32)
+            for i in range(CHUNK // PAIR):
+                bank = psum_ring.tile([P, PAIR, 2, P], F32, tag="ring")
+                for jj in range(PAIR):
+                    words = x_sb[c][:, PAIR * i + jj, :].bitcast(F32)
                     for u in range(2):
                         nc.tensor.transpose(bank[:, jj, u, :], words[:, u : C // 2 : 2], identity[:])
                 banks.append(bank)
             return banks
 
         def regroup(banks):
-            grouped = stage.tile([P, J, P, PACK], BF16, align_bytes=64, tag="grouped")
-            for half in range(2):
+            grouped = stage.tile([P, CHUNK, P, PACK], BF16, align_bytes=64, tag="grouped")
+            for i in range(CHUNK // PAIR):
                 nc.vector.tensor_copy(
-                    out=grouped[:, 2 * half : 2 * half + 2]
+                    out=grouped[:, PAIR * i : PAIR * (i + 1)]
                     .rearrange("p j r t -> p (j r t)")
                     .bitcast(F32)
-                    .rearrange("p (j r u) -> p j r u", j=2, u=2),
-                    in_=banks[half][:].rearrange("p j u r -> p j r u"),
+                    .rearrange("p (j r u) -> p j r u", j=PAIR, u=2),
+                    in_=banks[i][:].rearrange("p j u r -> p j r u"),
                 )
             return grouped
 
-        def quantise(grouped):
-            codes = stage.tile([P, J * P], U32, align_bytes=64, tag="codes")
-            scales = stage.tile([P, J * P], U8, align_bytes=64, tag="scales")
+        x_codes = {}
+        x_scales = {}
+
+        def quantise(c, grouped):
+            group, j0 = c // 2, CHUNK * (c % 2)
+            if j0 == 0:
+                x_codes[group] = stage.tile([P, J * P], U32, align_bytes=64, tag="codes", name="codes")
+                x_scales[group] = stage.tile([P, J * P], U8, align_bytes=64, tag="scales", name="scales")
+            columns = slice(j0 * P, (j0 + CHUNK) * P)
             nc.vector.quantize_mx(
-                out=codes[:].bitcast(FP8X4),
-                scales=scales[:],
+                out=x_codes[group][:, columns].bitcast(FP8X4),
+                scales=x_scales[group][:, columns],
                 in_=grouped[:].rearrange("p j r t -> p (j r t)"),
             )
-            return codes, scales
 
-        def project(block, x_mx, j, pool, tag):
-            codes, scales = x_mx
-            acc = pool.tile([P, H, D], F32, tag=tag)
-            nc.tensor.matmul_mx(
-                out=acc[:].rearrange("p h d -> p (h d)"),
-                lhsT=codes[:, j * P : (j + 1) * P].bitcast(FP8X4),
-                lhsT_scale=scales[:, j * P : (j + 1) * P],
-                rhs=w_words[:, block * 2 * C : (block + 1) * 2 * C].bitcast(FP4X4),
-                rhs_scale=w_scales[:, block * C : (block + 1) * C],
-                start=True,
-                stop=True,
-            )
+        def project(block, rnd, i, pool, tag):
+            group, first_column = rnd // 2, block * C + (rnd % 2) * HR * D
+            acc = pool.tile([P, PAIR, HR, D], F32, tag=tag)
+            for jj in range(PAIR):
+                tokens = slice((PAIR * i + jj) * P, (PAIR * i + jj + 1) * P)
+                nc.tensor.matmul_mx(
+                    out=acc[:, jj].rearrange("p h d -> p (h d)"),
+                    lhsT=x_codes[group][:, tokens].bitcast(FP8X4),
+                    lhsT_scale=x_scales[group][:, tokens],
+                    rhs=w_words[:, 2 * first_column : 2 * (first_column + HR * D)].bitcast(FP4X4),
+                    rhs_scale=w_scales[:, first_column : first_column + HR * D],
+                    start=True,
+                    stop=True,
+                )
             return acc
 
-        def project_and_add_bias(block, x_mx, j, bias, res):
-            acc = project(block, x_mx, j, psum_ring, "ring")
-            nc.vector.tensor_tensor(out=res[:, :, j, :], in0=acc[:], in1=bias[:], op=ALU.add)
+        def like_bank(res, i):
+            return res[:, :, PAIR * i : PAIR * (i + 1)]
 
-        def sum_squares(rows, squares, sums, j):
-            for h in range(H):
-                nc.scalar.activation(
-                    out=squares[:, h, j, :], in_=rows[:, h, :], func=ACT.Square, accum_out=sums[:, h, j : j + 1]
-                )
-
-        head_halves = (slice(0, H // 2), slice(H // 2, H))
-
-        def store(dst, b, heads, res):
-            nc.sync.dma_start(
-                out=dst[b, heads].rearrange("h (p j) d -> p h (j d)", j=J),
-                in_=res[:, heads].rearrange("p h j d -> p h (j d)"),
+        def project_and_add_bias(block, rnd, i, bias, res):
+            acc = project(block, rnd, i, psum_ring, "ring")
+            heads = slice((rnd % 2) * HR, (rnd % 2 + 1) * HR)
+            nc.vector.tensor_tensor(
+                out=like_bank(res, i).rearrange("p h j d -> p j h d"),
+                in0=acc[:],
+                in1=bias[:, heads].unsqueeze(1).to_broadcast([P, PAIR, HR, D]),
+                op=ALU.add,
             )
 
-        def finish_q(b, q_res, q_scaled, second_engine):
-            q_factor = stage.tile([P, H, J], F32, tag="q_factor")
-            nc.scalar.activation(out=q_factor[:], in_=q_scaled[:], func=ACT.Abs_reciprocal_sqrt)
-            for engine, heads in zip((nc.gpsimd, second_engine), head_halves):
-                rows = q_res[:, heads].rearrange("p h j d -> p (h j) d")
-                factor = q_factor[:, heads].rearrange("p h j -> p (h j)").unsqueeze(2)
-                engine.tensor_tensor(out=rows, in0=rows, in1=factor.to_broadcast([P, H // 2 * J, D]), op=ALU.mult)
-                store(out_0, b, heads, q_res)
+        def sum_squares(rows_of_bank, squares, sums, i):
+            for jj in range(PAIR):
+                j = PAIR * i + jj
+                for h in range(HR):
+                    nc.scalar.activation(
+                        out=squares[:, h, j, :],
+                        in_=rows_of_bank[:, jj, h, :],
+                        func=ACT.Square,
+                        accum_out=sums[:, h, j : j + 1],
+                    )
 
-        x_mx = quantise(regroup(transpose_words(0)))
-        banks = transpose_words(1)
-        k_acc = [project(K, x_mx, j, psum_k, "k") for j in range(J)]
-        x_mx_next = None
+        def store(dst, rnd, h, res):
+            group, head = rnd // 2, (rnd % 2) * HR + h
+            nc.sync.dma_start(
+                out=dst[E * group : E * group + E, head].rearrange("e (s j) d -> s e (j d)", j=J),
+                in_=res[:, h].rearrange("p j d -> p (j d)"),
+            )
+
+        def inverse_sqrt(values, tag):
+            factor = stage.tile([P, HR, J], F32, tag=tag)
+            nc.scalar.activation(out=factor[:], in_=values[:], func=ACT.Abs_reciprocal_sqrt)
+            return factor
+
+        def scale_and_store_q(rnd, q_res, q_factor, second_engine):
+            for engine, h0 in ((nc.gpsimd, 0), (second_engine, HR // 2)):
+                heads = slice(h0, h0 + HR // 2)
+                rows_of_heads = q_res[:, heads].rearrange("p h j d -> p (h j) d")
+                factor = q_factor[:, heads].rearrange("p h j -> p (h j)").unsqueeze(2)
+                engine.tensor_tensor(
+                    out=rows_of_heads, in0=rows_of_heads, in1=factor.to_broadcast([P, HR // 2 * J, D]), op=ALU.mult
+                )
+                for h in range(h0, h0 + HR // 2):
+                    store(out_0, rnd, h, q_res)
+
+        grouped = regroup(transpose_words(0))
+        log_clamped = consts.tile([P, H], F32)
+        nc.vector.tensor_scalar_min(out=log_clamped[:], in0=spread(GAIN_ROW, D)[:, 0:H], scalar1=MAX_LOG_GAIN)
+        inv_gain_sq = consts.tile([P, H], F32)
+        nc.scalar.activation(out=inv_gain_sq[:], in_=log_clamped[:], func=ACT.Exp, scale=-2.0)
+        table_warm = consts.tile([P, H], F32)
+        nc.scalar.activation(out=table_warm[:], in_=inv_gain_sq[:], func=ACT.Abs_reciprocal_sqrt)
+        v_bias_sb = consts.tile([P, H, D], F32)
+        nc.scalar.copy(out=v_bias_sb[:].rearrange("p h d -> p (h d)"), in_=spread(V_ROW, C)[:])
+        q_bias_sb = consts.tile([P, H, D], F32)
+        nc.scalar.copy(out=q_bias_sb[:].rearrange("p h d -> p (h d)"), in_=spread(Q_ROW, C)[:])
+        quantise(0, grouped)
+        quantise(1, regroup(transpose_words(1)))
+        k_acc = [project(K, 0, i, psum_k, "k") for i in range(BANKS)]
+        banks = transpose_words(2)
         q_res = None
         q_scaled = None
+        q_factor = None
 
-        for b in range(B):
-            k_sums = stage.tile([P, H, J], F32, tag="k_sums")
-            k_squares = stage.tile([P, H, J, D], BF16, tag="k_squares")
+        for rnd in range(ROUNDS):
+            k_sums = stage.tile([P, HR, J], F32, tag="k_sums")
+            k_squares = stage.tile([P, HR, J, D], BF16, tag="k_squares")
             sum_squares(k_acc[0], k_squares, k_sums, 0)
-            if b > 0:
-                finish_q(b - 1, q_res, q_scaled, nc.gpsimd)
-            for j in range(1, J):
-                sum_squares(k_acc[j], k_squares, k_sums, j)
+            if rnd > 0:
+                q_factor = inverse_sqrt(q_scaled, "q_factor")
+            for i in range(1, BANKS):
+                sum_squares(k_acc[i], k_squares, k_sums, i)
 
-            if b + 1 < B:
+            if rnd + 2 < CHUNKS:
                 grouped = regroup(banks)
-            q_res = results.tile([P, H, J, D], F32, tag="q")
-            for j in range(J):
-                project_and_add_bias(Q, x_mx, j, q_bias_sb, q_res)
-            if b + 1 < B:
-                x_mx_next = quantise(grouped)
+            v_res = results.tile([P, HR, J, D], F32, tag="v")
+            for i in range(BANKS):
+                project_and_add_bias(V, rnd, i, v_bias_sb, v_res)
+            for h in range(HR):
+                store(out_2, rnd, h, v_res)
+            if rnd > 0:
+                scale_and_store_q(rnd - 1, q_res, q_factor, nc.gpsimd)
+            q_res = results.tile([P, HR, J, D], F32, tag="q")
+            for i in range(BANKS):
+                project_and_add_bias(Q, rnd, i, q_bias_sb, q_res)
+            if rnd + 3 < CHUNKS:
+                banks = transpose_words(rnd + 3)
 
-            q_sums = stage.tile([P, H, J], F32, tag="q_sums")
-            q_squares = stage.tile([P, H, J, D], BF16, tag="q_squares")
-            sum_squares(q_res[:, :, 0, :], q_squares, q_sums, 0)
-            k_clamped = stage.tile([P, H, J], F32, tag="k_clamped")
+            q_sums = stage.tile([P, HR, J], F32, tag="q_sums")
+            q_squares = stage.tile([P, HR, J, D], BF16, tag="q_squares")
+            sum_squares(like_bank(q_res, 0).rearrange("p h j d -> p j h d"), q_squares, q_sums, 0)
+            k_clamped = stage.tile([P, HR, J], F32, tag="k_clamped")
             nc.vector.tensor_scalar_max(out=k_clamped[:], in0=k_sums[:], scalar1=EPS * EPS)
-            k_factor = stage.tile([P, H, J], F32, tag="k_factor")
-            nc.scalar.activation(out=k_factor[:], in_=k_clamped[:], func=ACT.Abs_reciprocal_sqrt)
-            for j in range(1, J):
-                sum_squares(q_res[:, :, j, :], q_squares, q_sums, j)
+            k_factor = inverse_sqrt(k_clamped, "k_factor")
+            for i in range(1, BANKS):
+                sum_squares(like_bank(q_res, i).rearrange("p h j d -> p j h d"), q_squares, q_sums, i)
 
-            v_res = results.tile([P, H, J, D], F32, tag="v")
-            for j in range(J):
-                project_and_add_bias(V, x_mx, j, v_bias_sb, v_res)
-            for heads in head_halves:
-                store(out_2, b, heads, v_res)
-            if b + 2 < B:
-                banks = transpose_words(b + 2)
+            if rnd + 2 < CHUNKS:
+                quantise(rnd + 2, grouped)
 
-            k_res = results.tile([P, H, J, D], F32, tag="k")
-            for j in range(J):
+            k_res = results.tile([P, HR, J, D], F32, tag="k")
+            for i in range(BANKS):
                 nc.vector.tensor_tensor(
-                    out=k_res[:, :, j, :],
-                    in0=k_acc[j][:],
-                    in1=k_factor[:, :, j : j + 1].to_broadcast([P, H, D]),
+                    out=like_bank(k_res, i).rearrange("p h j d -> p j h d"),
+                    in0=k_acc[i][:],
+                    in1=like_bank(k_factor, i).rearrange("p h j -> p j h").unsqueeze(3).to_broadcast([P, PAIR, HR, D]),
                     op=ALU.mult,
                 )
-                if b + 1 < B:
-                    k_acc[j] = project(K, x_mx_next, j, psum_k, "k")
-            for heads in head_halves:
-                store(out_1, b, heads, k_res)
+                if rnd + 1 < ROUNDS:
+                    k_acc[i] = project(K, rnd + 1, i, psum_k, "k")
+            for h in range(HR):
+                store(out_1, rnd, h, k_res)
 
-            q_scaled = stage.tile([P, H, J], F32, tag="q_scaled")
+            heads = slice((rnd % 2) * HR, (rnd % 2 + 1) * HR)
+            q_scaled = stage.tile([P, HR, J], F32, tag="q_scaled")
             nc.vector.scalar_tensor_tensor(
                 out=q_scaled[:],
                 in0=q_sums[:],
                 scalar=EPS * EPS,
-                in1=inv_gain_sq[:].unsqueeze(2).to_broadcast([P, H, J]),
+                in1=inv_gain_sq[:, heads].unsqueeze(2).to_broadcast([P, HR, J]),
                 op0=ALU.max,
                 op1=ALU.mult,
             )
-            x_mx = x_mx_next
 
-        finish_q(B - 1, q_res, q_scaled, nc.vector)
+        scale_and_store_q(ROUNDS - 1, q_res, inverse_sqrt(q_scaled, "q_factor"), nc.vector)

@@ -13,6 +13,7 @@ FP8X4 = mybir.dt.float8_e4m3fn_x4
 FP4X4 = mybir.dt.float4_e2m1fn_x4
 ALU = mybir.AluOpType
 ACT = mybir.ActivationFunctionType
+AXIS = mybir.AxisListType
 
 B, L, C, H, D = 8, 512, 512, 8, 64
 P = 128
@@ -134,29 +135,40 @@ def tile_selfattention_pa_t_kernel(
                 )
             return acc
 
-        def like_bank(res, i):
-            return res[:, :, PAIR * i : PAIR * (i + 1)]
+        def rows_of_bank(res, i):
+            return res[:, :, PAIR * i : PAIR * (i + 1)].rearrange("p h j d -> p j h d")
 
-        def project_and_add_bias(block, rnd, i, bias, res):
-            acc = project(block, rnd, i, psum_ring, "ring")
+        def add_bias(acc, rnd, i, bias, res):
             heads = slice((rnd % 2) * HR, (rnd % 2 + 1) * HR)
             nc.vector.tensor_tensor(
-                out=like_bank(res, i).rearrange("p h j d -> p j h d"),
+                out=rows_of_bank(res, i),
                 in0=acc[:],
                 in1=bias[:, heads].unsqueeze(1).to_broadcast([P, PAIR, HR, D]),
                 op=ALU.add,
             )
 
-        def sum_squares(rows_of_bank, squares, sums, i):
+        def sum_squares(rows, squares, sums, i):
             for jj in range(PAIR):
                 j = PAIR * i + jj
                 for h in range(HR):
                     nc.scalar.activation(
                         out=squares[:, h, j, :],
-                        in_=rows_of_bank[:, jj, h, :],
+                        in_=rows[:, jj, h, :],
                         func=ACT.Square,
-                        accum_out=sums[:, h, j : j + 1],
+                        accum_out=sums[:, j, h : h + 1],
                     )
+
+        def fold_squares(rows):
+            squares = stage.tile([P, PAIR, HR, D], F32, tag="folded_squares")
+            nc.gpsimd.tensor_tensor(out=squares[:], in0=rows, in1=rows, op=ALU.mult)
+            for width in (D // 2, D // 4, D // 8):
+                nc.gpsimd.tensor_tensor(
+                    out=squares[:, :, :, 0:width],
+                    in0=squares[:, :, :, 0:width],
+                    in1=squares[:, :, :, width : 2 * width],
+                    op=ALU.add,
+                )
+            return squares[:, :, :, 0 : D // 8]
 
         def store(dst, rnd, h, res):
             group, head = rnd // 2, (rnd % 2) * HR + h
@@ -166,82 +178,87 @@ def tile_selfattention_pa_t_kernel(
             )
 
         def inverse_sqrt(values, tag):
-            factor = stage.tile([P, HR, J], F32, tag=tag)
+            factor = stage.tile([P, J, HR], F32, tag=tag)
             nc.scalar.activation(out=factor[:], in_=values[:], func=ACT.Abs_reciprocal_sqrt)
             return factor
 
-        def scale_and_store_q(rnd, q_res, q_factor, second_engine):
-            for engine, h0 in ((nc.gpsimd, 0), (second_engine, HR // 2)):
-                heads = slice(h0, h0 + HR // 2)
-                rows_of_heads = q_res[:, heads].rearrange("p h j d -> p (h j) d")
-                factor = q_factor[:, heads].rearrange("p h j -> p (h j)").unsqueeze(2)
-                engine.tensor_tensor(
-                    out=rows_of_heads, in0=rows_of_heads, in1=factor.to_broadcast([P, HR // 2 * J, D]), op=ALU.mult
-                )
-                for h in range(h0, h0 + HR // 2):
-                    store(out_0, rnd, h, q_res)
+        def scale_and_store_q(engine, rnd, half, q_res, q_factor):
+            heads = slice(half * HR // 2, (half + 1) * HR // 2)
+            factor = q_factor[:, :, heads].rearrange("p j h -> p h j").unsqueeze(3)
+            engine.tensor_tensor(
+                out=q_res[:, heads], in0=q_res[:, heads], in1=factor.to_broadcast([P, HR // 2, J, D]), op=ALU.mult
+            )
+            for h in range(half * HR // 2, (half + 1) * HR // 2):
+                store(out_0, rnd, h, q_res)
 
-        grouped = regroup(transpose_words(0))
         log_clamped = consts.tile([P, H], F32)
         nc.vector.tensor_scalar_min(out=log_clamped[:], in0=spread(GAIN_ROW, D)[:, 0:H], scalar1=MAX_LOG_GAIN)
         inv_gain_sq = consts.tile([P, H], F32)
         nc.scalar.activation(out=inv_gain_sq[:], in_=log_clamped[:], func=ACT.Exp, scale=-2.0)
         table_warm = consts.tile([P, H], F32)
         nc.scalar.activation(out=table_warm[:], in_=inv_gain_sq[:], func=ACT.Abs_reciprocal_sqrt)
+        quantise(0, regroup(transpose_words(0)))
         v_bias_sb = consts.tile([P, H, D], F32)
         nc.scalar.copy(out=v_bias_sb[:].rearrange("p h d -> p (h d)"), in_=spread(V_ROW, C)[:])
         q_bias_sb = consts.tile([P, H, D], F32)
         nc.scalar.copy(out=q_bias_sb[:].rearrange("p h d -> p (h d)"), in_=spread(Q_ROW, C)[:])
-        quantise(0, grouped)
         quantise(1, regroup(transpose_words(1)))
+        grouped = regroup(transpose_words(2))
         k_acc = [project(K, 0, i, psum_k, "k") for i in range(BANKS)]
-        banks = transpose_words(2)
         q_res = None
         q_scaled = None
         q_factor = None
 
         for rnd in range(ROUNDS):
-            k_sums = stage.tile([P, HR, J], F32, tag="k_sums")
+            k_sums = stage.tile([P, J, HR], F32, tag="k_sums")
             k_squares = stage.tile([P, HR, J, D], BF16, tag="k_squares")
             sum_squares(k_acc[0], k_squares, k_sums, 0)
             if rnd > 0:
                 q_factor = inverse_sqrt(q_scaled, "q_factor")
+                scale_and_store_q(nc.gpsimd, rnd - 1, 0, q_res, q_factor)
             for i in range(1, BANKS):
                 sum_squares(k_acc[i], k_squares, k_sums, i)
+            last_q_res = q_res
 
-            if rnd + 2 < CHUNKS:
-                grouped = regroup(banks)
-            v_res = results.tile([P, HR, J, D], F32, tag="v")
-            for i in range(BANKS):
-                project_and_add_bias(V, rnd, i, v_bias_sb, v_res)
-            for h in range(HR):
-                store(out_2, rnd, h, v_res)
-            if rnd > 0:
-                scale_and_store_q(rnd - 1, q_res, q_factor, nc.gpsimd)
             q_res = results.tile([P, HR, J, D], F32, tag="q")
             for i in range(BANKS):
-                project_and_add_bias(Q, rnd, i, q_bias_sb, q_res)
-            if rnd + 3 < CHUNKS:
-                banks = transpose_words(rnd + 3)
+                add_bias(project(Q, rnd, i, psum_ring, "ring"), rnd, i, q_bias_sb, q_res)
+            folded = fold_squares(rows_of_bank(q_res, 0))
+            if rnd > 0:
+                scale_and_store_q(nc.gpsimd, rnd - 1, 1, last_q_res, q_factor)
+            banks = transpose_words(rnd + 3) if rnd + 3 < CHUNKS else None
+            v_acc = [project(V, rnd, i, psum_ring, "ring") for i in range(BANKS)]
+            v_res = results.tile([P, HR, J, D], F32, tag="v")
 
-            q_sums = stage.tile([P, HR, J], F32, tag="q_sums")
+            def finish_v():
+                for i in range(BANKS):
+                    add_bias(v_acc[i], rnd, i, v_bias_sb, v_res)
+                for h in range(HR):
+                    store(out_2, rnd, h, v_res)
+
+            q_sums = stage.tile([P, J, HR], F32, tag="q_sums")
             q_squares = stage.tile([P, HR, J, D], BF16, tag="q_squares")
-            sum_squares(like_bank(q_res, 0).rearrange("p h j d -> p j h d"), q_squares, q_sums, 0)
-            k_clamped = stage.tile([P, HR, J], F32, tag="k_clamped")
+            sum_squares(rows_of_bank(q_res, 1), q_squares, q_sums, 1)
+            k_clamped = stage.tile([P, J, HR], F32, tag="k_clamped")
             nc.vector.tensor_scalar_max(out=k_clamped[:], in0=k_sums[:], scalar1=EPS * EPS)
             k_factor = inverse_sqrt(k_clamped, "k_factor")
-            for i in range(1, BANKS):
-                sum_squares(like_bank(q_res, i).rearrange("p h j d -> p j h d"), q_squares, q_sums, i)
+            for i in range(2, BANKS):
+                sum_squares(rows_of_bank(q_res, i), q_squares, q_sums, i)
 
-            if rnd + 2 < CHUNKS:
+            x_work_left = rnd + 2 < CHUNKS
+            if x_work_left:
                 quantise(rnd + 2, grouped)
+                if banks is not None:
+                    grouped = regroup(banks)
+            else:
+                finish_v()
 
             k_res = results.tile([P, HR, J, D], F32, tag="k")
             for i in range(BANKS):
                 nc.vector.tensor_tensor(
-                    out=like_bank(k_res, i).rearrange("p h j d -> p j h d"),
+                    out=rows_of_bank(k_res, i),
                     in0=k_acc[i][:],
-                    in1=like_bank(k_factor, i).rearrange("p h j -> p j h").unsqueeze(3).to_broadcast([P, PAIR, HR, D]),
+                    in1=k_factor[:, PAIR * i : PAIR * (i + 1), :].unsqueeze(3).to_broadcast([P, PAIR, HR, D]),
                     op=ALU.mult,
                 )
                 if rnd + 1 < ROUNDS:
@@ -249,15 +266,20 @@ def tile_selfattention_pa_t_kernel(
             for h in range(HR):
                 store(out_1, rnd, h, k_res)
 
+            nc.vector.tensor_reduce(out=q_sums[:, 0:PAIR, :], in_=folded, axis=AXIS.X, op=ALU.add)
             heads = slice((rnd % 2) * HR, (rnd % 2 + 1) * HR)
-            q_scaled = stage.tile([P, HR, J], F32, tag="q_scaled")
+            q_scaled = stage.tile([P, J, HR], F32, tag="q_scaled")
             nc.vector.scalar_tensor_tensor(
                 out=q_scaled[:],
                 in0=q_sums[:],
                 scalar=EPS * EPS,
-                in1=inv_gain_sq[:, heads].unsqueeze(2).to_broadcast([P, HR, J]),
+                in1=inv_gain_sq[:, heads].unsqueeze(1).to_broadcast([P, J, HR]),
                 op0=ALU.max,
                 op1=ALU.mult,
             )
+            if x_work_left:
+                finish_v()
 
-        scale_and_store_q(ROUNDS - 1, q_res, inverse_sqrt(q_scaled, "q_factor"), nc.vector)
+        q_factor = inverse_sqrt(q_scaled, "q_factor")
+        scale_and_store_q(nc.gpsimd, ROUNDS - 1, 0, q_res, q_factor)
+        scale_and_store_q(nc.vector, ROUNDS - 1, 1, q_res, q_factor)

@@ -13,7 +13,6 @@ FP8X4 = mybir.dt.float8_e4m3fn_x4
 FP4X4 = mybir.dt.float4_e2m1fn_x4
 ALU = mybir.AluOpType
 ACT = mybir.ActivationFunctionType
-AXIS = mybir.AxisListType
 
 B, L, C, H, D = 8, 512, 512, 8, 64
 P = 128
@@ -135,40 +134,29 @@ def tile_selfattention_pa_t_kernel(
                 )
             return acc
 
-        def rows_of_bank(res, i):
-            return res[:, :, PAIR * i : PAIR * (i + 1)].rearrange("p h j d -> p j h d")
+        def like_bank(res, i):
+            return res[:, :, PAIR * i : PAIR * (i + 1)]
 
-        def add_bias(acc, rnd, i, bias, res):
+        def project_and_add_bias(block, rnd, i, bias, res):
+            acc = project(block, rnd, i, psum_ring, "ring")
             heads = slice((rnd % 2) * HR, (rnd % 2 + 1) * HR)
             nc.vector.tensor_tensor(
-                out=rows_of_bank(res, i),
+                out=like_bank(res, i).rearrange("p h j d -> p j h d"),
                 in0=acc[:],
                 in1=bias[:, heads].unsqueeze(1).to_broadcast([P, PAIR, HR, D]),
                 op=ALU.add,
             )
 
-        def sum_squares(rows, squares, sums, i):
+        def sum_squares(rows_of_bank, squares, sums, i):
             for jj in range(PAIR):
                 j = PAIR * i + jj
                 for h in range(HR):
                     nc.scalar.activation(
                         out=squares[:, h, j, :],
-                        in_=rows[:, jj, h, :],
+                        in_=rows_of_bank[:, jj, h, :],
                         func=ACT.Square,
-                        accum_out=sums[:, j, h : h + 1],
+                        accum_out=sums[:, h, j : j + 1],
                     )
-
-        def fold_squares(rows):
-            squares = stage.tile([P, PAIR, HR, D], F32, tag="folded_squares")
-            nc.gpsimd.tensor_tensor(out=squares[:], in0=rows, in1=rows, op=ALU.mult)
-            for width in (D // 2, D // 4, D // 8):
-                nc.gpsimd.tensor_tensor(
-                    out=squares[:, :, :, 0:width],
-                    in0=squares[:, :, :, 0:width],
-                    in1=squares[:, :, :, width : 2 * width],
-                    op=ALU.add,
-                )
-            return squares[:, :, :, 0 : D // 8]
 
         def store(dst, rnd, h, res):
             group, head = rnd // 2, (rnd % 2) * HR + h
@@ -178,87 +166,84 @@ def tile_selfattention_pa_t_kernel(
             )
 
         def inverse_sqrt(values, tag):
-            factor = stage.tile([P, J, HR], F32, tag=tag)
+            factor = stage.tile([P, HR, J], F32, tag=tag)
             nc.scalar.activation(out=factor[:], in_=values[:], func=ACT.Abs_reciprocal_sqrt)
             return factor
 
-        def scale_and_store_q(engine, rnd, half, q_res, q_factor):
-            heads = slice(half * HR // 2, (half + 1) * HR // 2)
-            factor = q_factor[:, :, heads].rearrange("p j h -> p h j").unsqueeze(3)
-            engine.tensor_tensor(
-                out=q_res[:, heads], in0=q_res[:, heads], in1=factor.to_broadcast([P, HR // 2, J, D]), op=ALU.mult
-            )
-            for h in range(half * HR // 2, (half + 1) * HR // 2):
-                store(out_0, rnd, h, q_res)
+        def scale_and_store_q(rnd, q_res, q_factor, second_engine):
+            for engine, h0 in ((nc.gpsimd, 0), (second_engine, HR // 2)):
+                heads = slice(h0, h0 + HR // 2)
+                rows_of_heads = q_res[:, heads].rearrange("p h j d -> p (h j) d")
+                factor = q_factor[:, heads].rearrange("p h j -> p (h j)").unsqueeze(2)
+                engine.tensor_tensor(
+                    out=rows_of_heads, in0=rows_of_heads, in1=factor.to_broadcast([P, HR // 2 * J, D]), op=ALU.mult
+                )
+                for h in range(h0, h0 + HR // 2):
+                    store(out_0, rnd, h, q_res)
 
-        log_clamped = consts.tile([P, H], F32)
-        nc.vector.tensor_scalar_min(out=log_clamped[:], in0=spread(GAIN_ROW, D)[:, 0:H], scalar1=MAX_LOG_GAIN)
-        inv_gain_sq = consts.tile([P, H], F32)
-        nc.scalar.activation(out=inv_gain_sq[:], in_=log_clamped[:], func=ACT.Exp, scale=-2.0)
-        table_warm = consts.tile([P, H], F32)
-        nc.scalar.activation(out=table_warm[:], in_=inv_gain_sq[:], func=ACT.Abs_reciprocal_sqrt)
-        quantise(0, regroup(transpose_words(0)))
+        grouped = regroup(transpose_words(0))
+        log_gain_bank = spread(GAIN_ROW, D)
         v_bias_sb = consts.tile([P, H, D], F32)
         nc.scalar.copy(out=v_bias_sb[:].rearrange("p h d -> p (h d)"), in_=spread(V_ROW, C)[:])
         q_bias_sb = consts.tile([P, H, D], F32)
         nc.scalar.copy(out=q_bias_sb[:].rearrange("p h d -> p (h d)"), in_=spread(Q_ROW, C)[:])
+        log_clamped = consts.tile([P, H], F32)
+        nc.vector.tensor_scalar_min(out=log_clamped[:], in0=log_gain_bank[:, 0:H], scalar1=MAX_LOG_GAIN)
+        inv_gain_sq = consts.tile([P, H], F32)
+        nc.scalar.activation(out=inv_gain_sq[:], in_=log_clamped[:], func=ACT.Exp, scale=-2.0)
+        table_warm = consts.tile([P, H], F32)
+        nc.scalar.activation(out=table_warm[:], in_=inv_gain_sq[:], func=ACT.Abs_reciprocal_sqrt)
+        quantise(0, grouped)
         quantise(1, regroup(transpose_words(1)))
-        grouped = regroup(transpose_words(2))
+        banks = transpose_words(2)
         k_acc = [project(K, 0, i, psum_k, "k") for i in range(BANKS)]
         q_res = None
         q_scaled = None
         q_factor = None
 
         for rnd in range(ROUNDS):
-            k_sums = stage.tile([P, J, HR], F32, tag="k_sums")
+            k_sums = stage.tile([P, HR, J], F32, tag="k_sums")
             k_squares = stage.tile([P, HR, J, D], BF16, tag="k_squares")
             sum_squares(k_acc[0], k_squares, k_sums, 0)
             if rnd > 0:
                 q_factor = inverse_sqrt(q_scaled, "q_factor")
-                scale_and_store_q(nc.gpsimd, rnd - 1, 0, q_res, q_factor)
             for i in range(1, BANKS):
                 sum_squares(k_acc[i], k_squares, k_sums, i)
-            last_q_res = q_res
 
-            q_res = results.tile([P, HR, J, D], F32, tag="q")
-            for i in range(BANKS):
-                add_bias(project(Q, rnd, i, psum_ring, "ring"), rnd, i, q_bias_sb, q_res)
-            folded = fold_squares(rows_of_bank(q_res, 0))
-            if rnd > 0:
-                scale_and_store_q(nc.gpsimd, rnd - 1, 1, last_q_res, q_factor)
-            banks = transpose_words(rnd + 3) if rnd + 3 < CHUNKS else None
-            v_acc = [project(V, rnd, i, psum_ring, "ring") for i in range(BANKS)]
+            if rnd + 2 < CHUNKS:
+                grouped = regroup(banks)
             v_res = results.tile([P, HR, J, D], F32, tag="v")
-
-            def finish_v():
-                for i in range(BANKS):
-                    add_bias(v_acc[i], rnd, i, v_bias_sb, v_res)
-                for h in range(HR):
-                    store(out_2, rnd, h, v_res)
-
-            q_sums = stage.tile([P, J, HR], F32, tag="q_sums")
-            q_squares = stage.tile([P, HR, J, D], BF16, tag="q_squares")
-            sum_squares(rows_of_bank(q_res, 1), q_squares, q_sums, 1)
-            k_clamped = stage.tile([P, J, HR], F32, tag="k_clamped")
+            for i in range(BANKS):
+                project_and_add_bias(V, rnd, i, v_bias_sb, v_res)
+            for h in range(HR):
+                store(out_2, rnd, h, v_res)
+            if rnd > 0:
+                scale_and_store_q(rnd - 1, q_res, q_factor, nc.gpsimd)
+            q_res = results.tile([P, HR, J, D], F32, tag="q")
+            for i in range(BANKS - 1):
+                project_and_add_bias(Q, rnd, i, q_bias_sb, q_res)
+            k_clamped = stage.tile([P, HR, J], F32, tag="k_clamped")
             nc.vector.tensor_scalar_max(out=k_clamped[:], in0=k_sums[:], scalar1=EPS * EPS)
-            k_factor = inverse_sqrt(k_clamped, "k_factor")
-            for i in range(2, BANKS):
-                sum_squares(rows_of_bank(q_res, i), q_squares, q_sums, i)
+            project_and_add_bias(Q, rnd, BANKS - 1, q_bias_sb, q_res)
+            if rnd + 3 < CHUNKS:
+                banks = transpose_words(rnd + 3)
 
-            x_work_left = rnd + 2 < CHUNKS
-            if x_work_left:
+            q_sums = stage.tile([P, HR, J], F32, tag="q_sums")
+            q_squares = stage.tile([P, HR, J, D], BF16, tag="q_squares")
+            sum_squares(like_bank(q_res, 0).rearrange("p h j d -> p j h d"), q_squares, q_sums, 0)
+            k_factor = inverse_sqrt(k_clamped, "k_factor")
+            for i in range(1, BANKS):
+                sum_squares(like_bank(q_res, i).rearrange("p h j d -> p j h d"), q_squares, q_sums, i)
+
+            if rnd + 2 < CHUNKS:
                 quantise(rnd + 2, grouped)
-                if banks is not None:
-                    grouped = regroup(banks)
-            else:
-                finish_v()
 
             k_res = results.tile([P, HR, J, D], F32, tag="k")
             for i in range(BANKS):
                 nc.vector.tensor_tensor(
-                    out=rows_of_bank(k_res, i),
+                    out=like_bank(k_res, i).rearrange("p h j d -> p j h d"),
                     in0=k_acc[i][:],
-                    in1=k_factor[:, PAIR * i : PAIR * (i + 1), :].unsqueeze(3).to_broadcast([P, PAIR, HR, D]),
+                    in1=like_bank(k_factor, i).rearrange("p h j -> p j h").unsqueeze(3).to_broadcast([P, PAIR, HR, D]),
                     op=ALU.mult,
                 )
                 if rnd + 1 < ROUNDS:
@@ -266,20 +251,15 @@ def tile_selfattention_pa_t_kernel(
             for h in range(HR):
                 store(out_1, rnd, h, k_res)
 
-            nc.vector.tensor_reduce(out=q_sums[:, 0:PAIR, :], in_=folded, axis=AXIS.X, op=ALU.add)
             heads = slice((rnd % 2) * HR, (rnd % 2 + 1) * HR)
-            q_scaled = stage.tile([P, J, HR], F32, tag="q_scaled")
+            q_scaled = stage.tile([P, HR, J], F32, tag="q_scaled")
             nc.vector.scalar_tensor_tensor(
                 out=q_scaled[:],
                 in0=q_sums[:],
                 scalar=EPS * EPS,
-                in1=inv_gain_sq[:, heads].unsqueeze(1).to_broadcast([P, J, HR]),
+                in1=inv_gain_sq[:, heads].unsqueeze(2).to_broadcast([P, HR, J]),
                 op0=ALU.max,
                 op1=ALU.mult,
             )
-            if x_work_left:
-                finish_v()
 
-        q_factor = inverse_sqrt(q_scaled, "q_factor")
-        scale_and_store_q(nc.gpsimd, ROUNDS - 1, 0, q_res, q_factor)
-        scale_and_store_q(nc.vector, ROUNDS - 1, 1, q_res, q_factor)
+        scale_and_store_q(ROUNDS - 1, q_res, inverse_sqrt(q_scaled, "q_factor"), nc.vector)

@@ -165,10 +165,15 @@ def tile_selfattention_pa_t_kernel(
                 in_=res[:, h].rearrange("p j d -> p (j d)"),
             )
 
-        def inverse_sqrt(values, tag):
+        def inverse_sqrt(values, tag, bias=0.0):
             factor = stage.tile([P, HR, J], F32, tag=tag)
-            nc.scalar.activation(out=factor[:], in_=values[:], func=ACT.Abs_reciprocal_sqrt)
+            nc.scalar.activation(out=factor[:], in_=values[:], func=ACT.Abs_reciprocal_sqrt, bias=bias)
             return factor
+
+        def excess(sums, tag):
+            over = stage.tile([P, HR, J], F32, tag=tag)
+            nc.scalar.activation(out=over[:], in_=sums[:], func=ACT.Relu, bias=-EPS * EPS)
+            return over
 
         def scale_and_store_q(rnd, q_res, q_factor, second_engine):
             for engine, h0 in ((nc.gpsimd, 0), (second_engine, HR // 2)):
@@ -209,6 +214,7 @@ def tile_selfattention_pa_t_kernel(
                 q_factor = inverse_sqrt(q_scaled, "q_factor")
             for i in range(1, BANKS):
                 sum_squares(k_acc[i], k_squares, k_sums, i)
+            k_over = excess(k_sums, "k_over")
 
             if rnd + 2 < CHUNKS:
                 grouped = regroup(banks)
@@ -220,18 +226,15 @@ def tile_selfattention_pa_t_kernel(
             if rnd > 0:
                 scale_and_store_q(rnd - 1, q_res, q_factor, nc.gpsimd)
             q_res = results.tile([P, HR, J, D], F32, tag="q")
-            for i in range(BANKS - 1):
+            for i in range(BANKS):
                 project_and_add_bias(Q, rnd, i, q_bias_sb, q_res)
-            k_clamped = stage.tile([P, HR, J], F32, tag="k_clamped")
-            nc.vector.tensor_scalar_max(out=k_clamped[:], in0=k_sums[:], scalar1=EPS * EPS)
-            project_and_add_bias(Q, rnd, BANKS - 1, q_bias_sb, q_res)
             if rnd + 3 < CHUNKS:
                 banks = transpose_words(rnd + 3)
 
             q_sums = stage.tile([P, HR, J], F32, tag="q_sums")
             q_squares = stage.tile([P, HR, J, D], BF16, tag="q_squares")
             sum_squares(like_bank(q_res, 0).rearrange("p h j d -> p j h d"), q_squares, q_sums, 0)
-            k_factor = inverse_sqrt(k_clamped, "k_factor")
+            k_factor = inverse_sqrt(k_over, "k_factor", bias=EPS * EPS)
             for i in range(1, BANKS):
                 sum_squares(like_bank(q_res, i).rearrange("p h j d -> p j h d"), q_squares, q_sums, i)
 

@@ -175,15 +175,15 @@ def tile_selfattention_pa_t_kernel(
             nc.scalar.activation(out=over[:], in_=sums[:], func=ACT.Relu, bias=-EPS * EPS)
             return over
 
-        def scale_and_store_q(rnd, q_res, q_factor, second_engine):
-            for engine, h0 in ((nc.gpsimd, 0), (second_engine, HR // 2)):
-                heads = slice(h0, h0 + HR // 2)
+        def scale_and_store_q(rnd, q_res, q_factor, engine, heads_at_once):
+            for h0 in range(0, HR, heads_at_once):
+                heads = slice(h0, h0 + heads_at_once)
                 rows_of_heads = q_res[:, heads].rearrange("p h j d -> p (h j) d")
                 factor = q_factor[:, heads].rearrange("p h j -> p (h j)").unsqueeze(2)
                 engine.tensor_tensor(
-                    out=rows_of_heads, in0=rows_of_heads, in1=factor.to_broadcast([P, HR // 2 * J, D]), op=ALU.mult
+                    out=rows_of_heads, in0=rows_of_heads, in1=factor.to_broadcast([P, heads_at_once * J, D]), op=ALU.mult
                 )
-                for h in range(h0, h0 + HR // 2):
+                for h in range(h0, h0 + heads_at_once):
                     store(out_0, rnd, h, q_res)
 
         grouped = regroup(transpose_words(0))
@@ -224,7 +224,7 @@ def tile_selfattention_pa_t_kernel(
             for h in range(HR):
                 store(out_2, rnd, h, v_res)
             if rnd > 0:
-                scale_and_store_q(rnd - 1, q_res, q_factor, nc.gpsimd)
+                scale_and_store_q(rnd - 1, q_res, q_factor, nc.gpsimd, HR // 2)
             q_res = results.tile([P, HR, J, D], F32, tag="q")
             for i in range(BANKS):
                 project_and_add_bias(Q, rnd, i, q_bias_sb, q_res)
@@ -265,4 +265,4 @@ def tile_selfattention_pa_t_kernel(
                 op1=ALU.mult,
             )
 
-        scale_and_store_q(ROUNDS - 1, q_res, inverse_sqrt(q_scaled, "q_factor"), nc.vector)
+        scale_and_store_q(ROUNDS - 1, q_res, inverse_sqrt(q_scaled, "q_factor"), nc.vector, 1)

@@ -26,7 +26,7 @@ ROUNDS = (B // E) * (H // HR)
 PAIR = 2
 BANKS = J // PAIR
 Q, K, V = 0, 1, 2
-GAIN_ROW, V_ROW, Q_ROW = 0, 1, 2
+V_ROW, Q_ROW = 0, 1
 EPS = 1e-12
 MAX_LOG_GAIN = math.log(100.0)
 FLOPS = 2 * B * L * C * 3 * C
@@ -51,12 +51,18 @@ def tile_selfattention_pa_t_kernel(
             tokens = x[E * group : E * group + E].rearrange("e (s j) c -> s e j c", j=J)
             nc.sync.dma_start(out=x_sb[c][:], in_=tokens[:, :, j0 : j0 + CHUNK, :])
 
+        gain_row = consts.tile([P, D], BF16)
+        nc.vector.memset(gain_row[:].bitcast(I32), 0)
+        nc.sync.dma_start(out=gain_row[0:1, 0:H], in_=log_scale_mul.rearrange("a h b c -> (a b c) h"))
         load_x(0)
-        small_rows = consts.tile([P, 3, C], BF16)
-        nc.vector.memset(small_rows[:].rearrange("p r c -> p (r c)").bitcast(I32), 0)
-        nc.sync.dma_start(out=small_rows[0:1, GAIN_ROW, 0:H], in_=log_scale_mul.rearrange("a h b c -> (a b c) h"))
-        nc.sync.dma_start(out=small_rows[0:1, V_ROW, :], in_=v_bias.unsqueeze(0))
-        nc.sync.dma_start(out=small_rows[0:1, Q_ROW, :], in_=q_bias.unsqueeze(0))
+        load_x(1)
+        ones = consts.tile([P, P], BF16)
+        nc.vector.memset(ones[:], 1.0)
+        bias_rows = consts.tile([P, 2, C], BF16)
+        nc.vector.memset(bias_rows[:].rearrange("p r c -> p (r c)").bitcast(I32), 0)
+        nc.sync.dma_start(out=bias_rows[0:1, V_ROW, :], in_=v_bias.unsqueeze(0))
+        w_words = consts.tile([P, 2 * 3 * C], U8, align_bytes=64)
+        nc.sync.dma_start(out=w_words[:].bitcast(I32), in_=W_qkv_words[0].bitcast(I32))
         w_scales = consts.tile([P, 3 * C], U8, align_bytes=64)
         nc.vector.memset(w_scales[:].bitcast(I32), 0)
         for quadrant in range(4):
@@ -64,20 +70,15 @@ def tile_selfattention_pa_t_kernel(
                 out=w_scales[32 * quadrant : 32 * quadrant + 4, :].bitcast(I32),
                 in_=W_qkv_scales[0, 4 * quadrant : 4 * quadrant + 4, :].bitcast(I32),
             )
-        w_words = consts.tile([P, 2 * 3 * C], U8, align_bytes=64)
-        nc.sync.dma_start(out=w_words[:].bitcast(I32), in_=W_qkv_words[0].bitcast(I32))
-        for c in range(1, CHUNKS):
+        nc.sync.dma_start(out=bias_rows[0:1, Q_ROW, :], in_=q_bias.unsqueeze(0))
+        for c in range(2, CHUNKS):
             load_x(c)
-
         identity = consts.tile([P, P], F32)
         make_identity(nc, identity[:])
 
-        ones = consts.tile([P, P], BF16)
-        nc.vector.memset(ones[:], 1.0)
-
-        def spread(row, width):
+        def spread(row):
             bank = psum_ring.tile([P, C], F32, tag="ring")
-            nc.tensor.matmul(out=bank[:, 0:width], lhsT=ones[:], rhs=small_rows[:, row, 0:width], start=True, stop=True)
+            nc.tensor.matmul(out=bank[:, 0 : row.shape[1]], lhsT=ones[:], rhs=row, start=True, stop=True)
             return bank
 
         def transpose_words(c):
@@ -91,10 +92,10 @@ def tile_selfattention_pa_t_kernel(
                 banks.append(bank)
             return banks
 
-        def regroup(banks):
+        def regroup(banks, copy):
             grouped = stage.tile([P, CHUNK, P, PACK], BF16, align_bytes=64, tag="grouped")
             for i in range(CHUNK // PAIR):
-                nc.vector.tensor_copy(
+                copy(
                     out=grouped[:, PAIR * i : PAIR * (i + 1)]
                     .rearrange("p j r t -> p (j r t)")
                     .bitcast(F32)
@@ -137,8 +138,7 @@ def tile_selfattention_pa_t_kernel(
         def like_bank(res, i):
             return res[:, :, PAIR * i : PAIR * (i + 1)]
 
-        def project_and_add_bias(block, rnd, i, bias, res):
-            acc = project(block, rnd, i, psum_ring, "ring")
+        def add_bias(acc, rnd, i, bias, res):
             heads = slice((rnd % 2) * HR, (rnd % 2 + 1) * HR)
             nc.vector.tensor_tensor(
                 out=like_bank(res, i).rearrange("p h j d -> p j h d"),
@@ -186,27 +186,47 @@ def tile_selfattention_pa_t_kernel(
                 for h in range(h0, h0 + heads_at_once):
                     store(out_0, rnd, h, q_res)
 
-        grouped = regroup(transpose_words(0))
-        log_gain_bank = spread(GAIN_ROW, D)
-        v_bias_sb = consts.tile([P, H, D], F32)
-        nc.scalar.copy(out=v_bias_sb[:].rearrange("p h d -> p (h d)"), in_=spread(V_ROW, C)[:])
-        q_bias_sb = consts.tile([P, H, D], F32)
-        nc.scalar.copy(out=q_bias_sb[:].rearrange("p h d -> p (h d)"), in_=spread(Q_ROW, C)[:])
-        log_clamped = consts.tile([P, H], F32)
-        nc.vector.tensor_scalar_min(out=log_clamped[:], in0=log_gain_bank[:, 0:H], scalar1=MAX_LOG_GAIN)
-        inv_gain_sq = consts.tile([P, H], F32)
-        nc.scalar.activation(out=inv_gain_sq[:], in_=log_clamped[:], func=ACT.Exp, scale=-2.0)
         table_warm = consts.tile([P, H], F32)
-        nc.scalar.activation(out=table_warm[:], in_=inv_gain_sq[:], func=ACT.Abs_reciprocal_sqrt)
+        nc.scalar.activation(out=table_warm[:], in_=ones[:, 0:H], func=ACT.Exp)
+        inv_gain_sq_raw = consts.tile([P, H], F32)
+        nc.scalar.activation(out=inv_gain_sq_raw[:], in_=spread(gain_row[:])[:, 0:H], func=ACT.Exp, scale=-2.0)
+        nc.scalar.activation(out=table_warm[:], in_=inv_gain_sq_raw[:], func=ACT.Abs_reciprocal_sqrt)
+        inv_gain_sq = consts.tile([P, H], F32)
+        nc.gpsimd.tensor_scalar(
+            out=inv_gain_sq[:], in0=inv_gain_sq_raw[:], scalar1=math.exp(-2.0 * MAX_LOG_GAIN), scalar2=None, op0=ALU.max
+        )
+        grouped = regroup(transpose_words(0), nc.vector.tensor_copy)
+        v_bias_sb = consts.tile([P, H, D], F32)
+        nc.scalar.copy(out=v_bias_sb[:].rearrange("p h d -> p (h d)"), in_=spread(bias_rows[:, V_ROW, :])[:])
+        grouped_1 = regroup(transpose_words(1), nc.scalar.copy)
         quantise(0, grouped)
-        quantise(1, regroup(transpose_words(1)))
-        banks = transpose_words(2)
-        k_acc = [project(K, 0, i, psum_k, "k") for i in range(BANKS)]
+
+        def v_banks(rnd, v_res, some_banks):
+            for i in some_banks:
+                add_bias(project(V, rnd, i, psum_ring, "ring"), rnd, i, v_bias_sb, v_res)
+
+        v_res = results.tile([P, HR, J, D], F32, tag="v")
+        v_banks(0, v_res, range(0, BANKS // 2))
+        q_bias_sb = consts.tile([P, H, D], F32)
+        nc.scalar.copy(out=q_bias_sb[:].rearrange("p h d -> p (h d)"), in_=spread(bias_rows[:, Q_ROW, :])[:])
+        k_acc = [project(K, 0, i, psum_k, "k") for i in range(0, BANKS // 2)]
+        quantise(1, grouped_1)
+        v_banks(0, v_res, range(BANKS // 2, BANKS))
+        k_acc.extend([project(K, 0, i, psum_k, "k") for i in range(BANKS // 2, BANKS)])
+        banks = None
         q_res = None
         q_scaled = None
         q_factor = None
 
         for rnd in range(ROUNDS):
+            if rnd > 0:
+                if rnd + 2 < CHUNKS:
+                    grouped = regroup(banks, nc.vector.tensor_copy)
+                v_res = results.tile([P, HR, J, D], F32, tag="v")
+                v_banks(rnd, v_res, range(BANKS))
+            for h in range(HR):
+                store(out_2, rnd, h, v_res)
+
             k_sums = stage.tile([P, HR, J], F32, tag="k_sums")
             k_squares = stage.tile([P, HR, J, D], BF16, tag="k_squares")
             sum_squares(k_acc[0], k_squares, k_sums, 0)
@@ -215,19 +235,14 @@ def tile_selfattention_pa_t_kernel(
             for i in range(1, BANKS):
                 sum_squares(k_acc[i], k_squares, k_sums, i)
             k_over = excess(k_sums, "k_over")
-
-            if rnd + 2 < CHUNKS:
-                grouped = regroup(banks)
-            v_res = results.tile([P, HR, J, D], F32, tag="v")
-            for i in range(BANKS):
-                project_and_add_bias(V, rnd, i, v_bias_sb, v_res)
-            for h in range(HR):
-                store(out_2, rnd, h, v_res)
             if rnd > 0:
                 scale_and_store_q(rnd - 1, q_res, q_factor, nc.gpsimd, HR // 2)
+
+            if rnd == 0:
+                grouped = regroup(transpose_words(2), nc.vector.tensor_copy)
             q_res = results.tile([P, HR, J, D], F32, tag="q")
             for i in range(BANKS):
-                project_and_add_bias(Q, rnd, i, q_bias_sb, q_res)
+                add_bias(project(Q, rnd, i, psum_ring, "ring"), rnd, i, q_bias_sb, q_res)
             if rnd + 3 < CHUNKS:
                 banks = transpose_words(rnd + 3)
 

@@ -92,10 +92,10 @@ def tile_selfattention_pa_t_kernel(
                 banks.append(bank)
             return banks
 
-        def regroup(banks, copy):
+        def regroup(banks, copies):
             grouped = stage.tile([P, CHUNK, P, PACK], BF16, align_bytes=64, tag="grouped")
             for i in range(CHUNK // PAIR):
-                copy(
+                copies[i](
                     out=grouped[:, PAIR * i : PAIR * (i + 1)]
                     .rearrange("p j r t -> p (j r t)")
                     .bitcast(F32)
@@ -195,10 +195,10 @@ def tile_selfattention_pa_t_kernel(
         nc.gpsimd.tensor_scalar(
             out=inv_gain_sq[:], in0=inv_gain_sq_raw[:], scalar1=math.exp(-2.0 * MAX_LOG_GAIN), scalar2=None, op0=ALU.max
         )
-        grouped = regroup(transpose_words(0), nc.vector.tensor_copy)
+        grouped = regroup(transpose_words(0), (nc.vector.tensor_copy, nc.vector.tensor_copy))
         v_bias_sb = consts.tile([P, H, D], F32)
         nc.scalar.copy(out=v_bias_sb[:].rearrange("p h d -> p (h d)"), in_=spread(bias_rows[:, V_ROW, :])[:])
-        grouped_1 = regroup(transpose_words(1), nc.scalar.copy)
+        grouped_1 = regroup(transpose_words(1), (nc.scalar.copy, nc.scalar.copy))
         quantise(0, grouped)
 
         def v_banks(rnd, v_res, some_banks):
@@ -221,7 +221,7 @@ def tile_selfattention_pa_t_kernel(
         for rnd in range(ROUNDS):
             if rnd > 0:
                 if rnd + 2 < CHUNKS:
-                    grouped = regroup(banks, nc.vector.tensor_copy)
+                    grouped = regroup(banks, (nc.vector.tensor_copy, nc.scalar.copy))
                 v_res = results.tile([P, HR, J, D], F32, tag="v")
                 v_banks(rnd, v_res, range(BANKS))
             for h in range(HR):
@@ -239,7 +239,7 @@ def tile_selfattention_pa_t_kernel(
                 scale_and_store_q(rnd - 1, q_res, q_factor, nc.gpsimd, HR // 2)
 
             if rnd == 0:
-                grouped = regroup(transpose_words(2), nc.vector.tensor_copy)
+                grouped = regroup(transpose_words(2), (nc.vector.tensor_copy, nc.scalar.copy))
             q_res = results.tile([P, HR, J, D], F32, tag="q")
             for i in range(BANKS):
                 add_bias(project(Q, rnd, i, psum_ring, "ring"), rnd, i, q_bias_sb, q_res)
@@ -253,9 +253,6 @@ def tile_selfattention_pa_t_kernel(
             for i in range(1, BANKS):
                 sum_squares(like_bank(q_res, i).rearrange("p h j d -> p j h d"), q_squares, q_sums, i)
 
-            if rnd + 2 < CHUNKS:
-                quantise(rnd + 2, grouped)
-
             k_res = results.tile([P, HR, J, D], F32, tag="k")
             for i in range(BANKS):
                 nc.vector.tensor_tensor(
@@ -266,6 +263,8 @@ def tile_selfattention_pa_t_kernel(
                 )
                 if rnd + 1 < ROUNDS:
                     k_acc[i] = project(K, rnd + 1, i, psum_k, "k")
+                if i == BANKS // 2 - 1 and rnd + 2 < CHUNKS:
+                    quantise(rnd + 2, grouped)
             for h in range(HR):
                 store(out_1, rnd, h, k_res)
 

@@ -147,8 +147,8 @@ def tile_selfattention_pa_t_kernel(
                 op=ALU.add,
             )
 
-        def sum_squares(rows_of_bank, squares, sums, i):
-            for jj in range(PAIR):
+        def sum_squares(rows_of_bank, squares, sums, i, tiles_of_bank=range(PAIR)):
+            for jj in tiles_of_bank:
                 j = PAIR * i + jj
                 for h in range(HR):
                     nc.scalar.activation(
@@ -234,7 +234,6 @@ def tile_selfattention_pa_t_kernel(
                 q_factor = inverse_sqrt(q_scaled, "q_factor")
             for i in range(1, BANKS):
                 sum_squares(k_acc[i], k_squares, k_sums, i)
-            k_over = excess(k_sums, "k_over")
             if rnd > 0:
                 scale_and_store_q(rnd - 1, q_res, q_factor, nc.gpsimd, HR // 2)
 
@@ -248,7 +247,9 @@ def tile_selfattention_pa_t_kernel(
 
             q_sums = stage.tile([P, HR, J], F32, tag="q_sums")
             q_squares = stage.tile([P, HR, J, D], BF16, tag="q_squares")
-            sum_squares(like_bank(q_res, 0).rearrange("p h j d -> p j h d"), q_squares, q_sums, 0)
+            sum_squares(like_bank(q_res, 0).rearrange("p h j d -> p j h d"), q_squares, q_sums, 0, range(0, 1))
+            k_over = excess(k_sums, "k_over")
+            sum_squares(like_bank(q_res, 0).rearrange("p h j d -> p j h d"), q_squares, q_sums, 0, range(1, PAIR))
             k_factor = inverse_sqrt(k_over, "k_factor", bias=EPS * EPS)
             for i in range(1, BANKS):
                 sum_squares(like_bank(q_res, i).rearrange("p h j d -> p j h d"), q_squares, q_sums, i)

@@ -58,6 +58,8 @@ def tile_selfattention_pa_t_kernel(
         load_x(1)
         ones = consts.tile([P, P], BF16)
         nc.vector.memset(ones[:], 1.0)
+        warm_rows = consts.tile([P, C], BF16)
+        nc.vector.memset(warm_rows[:], 1.0)
         bias_rows = consts.tile([P, 2, C], BF16)
         nc.vector.memset(bias_rows[:].rearrange("p r c -> p (r c)").bitcast(I32), 0)
         nc.sync.dma_start(out=bias_rows[0:1, V_ROW, :], in_=v_bias.unsqueeze(0))
@@ -80,6 +82,11 @@ def tile_selfattention_pa_t_kernel(
             bank = psum_ring.tile([P, C], F32, tag="ring")
             nc.tensor.matmul(out=bank[:, 0 : row.shape[1]], lhsT=ones[:], rhs=row, start=True, stop=True)
             return bank
+
+        def warm_up(passes):
+            for i in range(passes):
+                bank = psum_ring.tile([P, C], F32, tag="ring", name="warm")
+                nc.tensor.matmul(out=bank[:], lhsT=ones[:], rhs=warm_rows[:], start=True, stop=True)
 
         def transpose_words(c):
             banks = []
@@ -188,8 +195,10 @@ def tile_selfattention_pa_t_kernel(
 
         table_warm = consts.tile([P, H], F32)
         nc.scalar.activation(out=table_warm[:], in_=ones[:, 0:H], func=ACT.Exp)
+        warm_up(3)
         inv_gain_sq_raw = consts.tile([P, H], F32)
         nc.scalar.activation(out=inv_gain_sq_raw[:], in_=spread(gain_row[:])[:, 0:H], func=ACT.Exp, scale=-2.0)
+        warm_up(2)
         nc.scalar.activation(out=table_warm[:], in_=inv_gain_sq_raw[:], func=ACT.Abs_reciprocal_sqrt)
         inv_gain_sq = consts.tile([P, H], F32)
         nc.gpsimd.tensor_scalar(

@@ -27,6 +27,20 @@ PAIR = 2
 BANKS = J // PAIR
 Q, K, V = 0, 1, 2
 V_ROW, Q_ROW = 0, 1
+GT = 1
+FOLD = ()
+S_BOTH = ()
+V_BOTH = ()
+V_Q = {}
+K_RED = ()
+G_SMALL = False
+EARLY = 0
+V_EARLY = 1
+Q_STORE_EARLY = True
+HALF_K = False
+RED_EARLY = 3
+FOLD_EARLY = True
+FOLDED = 16
 EPS = 1e-12
 MAX_LOG_GAIN = math.log(100.0)
 FLOPS = 2 * B * L * C * 3 * C
@@ -46,20 +60,20 @@ def tile_selfattention_pa_t_kernel(
 
         x_sb = [consts.tile([P, CHUNK, C], BF16, name="x_sb%d" % c) for c in range(CHUNKS)]
 
-        def load_x(c):
+        def load_x(c, tiles=range(CHUNK)):
             group, j0 = c // 2, CHUNK * (c % 2)
             tokens = x[E * group : E * group + E].rearrange("e (s j) c -> s e j c", j=J)
-            nc.sync.dma_start(out=x_sb[c][:], in_=tokens[:, :, j0 : j0 + CHUNK, :])
+            nc.sync.dma_start(
+                out=x_sb[c][:, tiles.start : tiles.stop, :], in_=tokens[:, :, j0 + tiles.start : j0 + tiles.stop, :]
+            )
 
         gain_row = consts.tile([P, D], BF16)
         nc.vector.memset(gain_row[:].bitcast(I32), 0)
         nc.sync.dma_start(out=gain_row[0:1, 0:H], in_=log_scale_mul.rearrange("a h b c -> (a b c) h"))
         load_x(0)
         load_x(1)
-        ones = consts.tile([P, P], BF16)
+        ones = consts.tile([P, C], BF16)
         nc.vector.memset(ones[:], 1.0)
-        warm_rows = consts.tile([P, C], BF16)
-        nc.vector.memset(warm_rows[:], 1.0)
         bias_rows = consts.tile([P, 2, C], BF16)
         nc.vector.memset(bias_rows[:].rearrange("p r c -> p (r c)").bitcast(I32), 0)
         nc.sync.dma_start(out=bias_rows[0:1, V_ROW, :], in_=v_bias.unsqueeze(0))
@@ -80,50 +94,56 @@ def tile_selfattention_pa_t_kernel(
 
         def spread(row):
             bank = psum_ring.tile([P, C], F32, tag="ring")
-            nc.tensor.matmul(out=bank[:, 0 : row.shape[1]], lhsT=ones[:], rhs=row, start=True, stop=True)
+            nc.tensor.matmul(out=bank[:, 0 : row.shape[1]], lhsT=ones[:, 0:P], rhs=row, start=True, stop=True)
             return bank
 
         def warm_up(passes):
             for i in range(passes):
                 bank = psum_ring.tile([P, C], F32, tag="ring", name="warm")
-                nc.tensor.matmul(out=bank[:], lhsT=ones[:], rhs=warm_rows[:], start=True, stop=True)
+                nc.tensor.matmul(out=bank[:], lhsT=ones[:, 0:P], rhs=ones[:], start=True, stop=True)
+
+        def transpose_bank(c, i):
+            bank = psum_ring.tile([P, PAIR, 2, P], F32, tag="ring")
+            for jj in range(PAIR):
+                words = x_sb[c][:, PAIR * i + jj, :].bitcast(F32)
+                for u in range(2):
+                    nc.tensor.transpose(bank[:, jj, u, :], words[:, u : C // 2 : 2], identity[:])
+            return bank
 
         def transpose_words(c):
-            banks = []
-            for i in range(CHUNK // PAIR):
-                bank = psum_ring.tile([P, PAIR, 2, P], F32, tag="ring")
-                for jj in range(PAIR):
-                    words = x_sb[c][:, PAIR * i + jj, :].bitcast(F32)
-                    for u in range(2):
-                        nc.tensor.transpose(bank[:, jj, u, :], words[:, u : C // 2 : 2], identity[:])
-                banks.append(bank)
-            return banks
+            return [transpose_bank(c, i) for i in range(CHUNK // PAIR)]
+
+        def new_grouped():
+            return stage.tile([P, CHUNK, P, PACK], BF16, align_bytes=64, tag="grouped", name="grouped")
+
+        def regroup_bank(grouped, i, bank, copy):
+            copy(
+                out=grouped[:, PAIR * i : PAIR * (i + 1)]
+                .rearrange("p j r t -> p (j r t)")
+                .bitcast(F32)
+                .rearrange("p (j r u) -> p j r u", j=PAIR, u=2),
+                in_=bank[:].rearrange("p j u r -> p j r u"),
+            )
 
         def regroup(banks, copies):
-            grouped = stage.tile([P, CHUNK, P, PACK], BF16, align_bytes=64, tag="grouped")
+            grouped = new_grouped()
             for i in range(CHUNK // PAIR):
-                copies[i](
-                    out=grouped[:, PAIR * i : PAIR * (i + 1)]
-                    .rearrange("p j r t -> p (j r t)")
-                    .bitcast(F32)
-                    .rearrange("p (j r u) -> p j r u", j=PAIR, u=2),
-                    in_=banks[i][:].rearrange("p j u r -> p j r u"),
-                )
+                regroup_bank(grouped, i, banks[i], copies[i])
             return grouped
 
         x_codes = {}
         x_scales = {}
 
-        def quantise(c, grouped):
+        def quantise(c, grouped, tiles=range(CHUNK)):
             group, j0 = c // 2, CHUNK * (c % 2)
-            if j0 == 0:
+            if j0 == 0 and tiles.start == 0:
                 x_codes[group] = stage.tile([P, J * P], U32, align_bytes=64, tag="codes", name="codes")
                 x_scales[group] = stage.tile([P, J * P], U8, align_bytes=64, tag="scales", name="scales")
-            columns = slice(j0 * P, (j0 + CHUNK) * P)
+            columns = slice((j0 + tiles.start) * P, (j0 + tiles.stop) * P)
             nc.vector.quantize_mx(
                 out=x_codes[group][:, columns].bitcast(FP8X4),
                 scales=x_scales[group][:, columns],
-                in_=grouped[:].rearrange("p j r t -> p (j r t)"),
+                in_=grouped[:, tiles.start : tiles.stop].rearrange("p j r t -> p (j r t)"),
             )
 
         def project(block, rnd, i, pool, tag):
@@ -165,6 +185,22 @@ def tile_selfattention_pa_t_kernel(
                         accum_out=sums[:, h, j : j + 1],
                     )
 
+        def q_tile(q_res, q_squares, q_sums, j):
+            sum_squares(
+                like_bank(q_res, j // PAIR).rearrange("p h j d -> p j h d"), q_squares, q_sums, j // PAIR, range(j % PAIR, j % PAIR + 1)
+            )
+
+        def fold_step(squares, q_res, width):
+            if width == D:
+                rows = q_res[:, :, 0:GT]
+                nc.gpsimd.tensor_tensor(out=squares[:], in0=rows, in1=rows, op=ALU.mult)
+            else:
+                low = squares[:, :, :, 0:width]
+                nc.gpsimd.tensor_tensor(out=low, in0=low, in1=squares[:, :, :, width : 2 * width], op=ALU.add)
+
+        def sum_folded(squares, sums):
+            nc.vector.tensor_reduce(out=sums[:, :, 0:GT], in_=squares[:, :, :, 0:FOLDED], axis=mybir.AxisListType.X, op=ALU.add)
+
         def store(dst, rnd, h, res):
             group, head = rnd // 2, (rnd % 2) * HR + h
             nc.sync.dma_start(
@@ -173,25 +209,35 @@ def tile_selfattention_pa_t_kernel(
             )
 
         def inverse_sqrt(values, tag, bias=0.0):
-            factor = stage.tile([P, HR, J], F32, tag=tag)
+            factor = stage.tile([P, HR, J], F32, tag=tag, name=tag)
             nc.scalar.activation(out=factor[:], in_=values[:], func=ACT.Abs_reciprocal_sqrt, bias=bias)
             return factor
 
         def excess(sums, tag):
-            over = stage.tile([P, HR, J], F32, tag=tag)
+            over = stage.tile([P, HR, J], F32, tag=tag, name=tag)
             nc.scalar.activation(out=over[:], in_=sums[:], func=ACT.Relu, bias=-EPS * EPS)
             return over
 
-        def scale_and_store_q(rnd, q_res, q_factor, engine, heads_at_once):
-            for h0 in range(0, HR, heads_at_once):
-                heads = slice(h0, h0 + heads_at_once)
-                rows_of_heads = q_res[:, heads].rearrange("p h j d -> p (h j) d")
-                factor = q_factor[:, heads].rearrange("p h j -> p (h j)").unsqueeze(2)
-                engine.tensor_tensor(
-                    out=rows_of_heads, in0=rows_of_heads, in1=factor.to_broadcast([P, heads_at_once * J, D]), op=ALU.mult
-                )
-                for h in range(h0, h0 + heads_at_once):
+        def scale_and_store_q(rnd, q_res, q_factor, engine, heads, at_once=1):
+            for h0 in heads[::at_once]:
+                some = slice(h0, h0 + at_once)
+                rows = q_res[:, some].rearrange("p h j d -> p (h j) d")
+                factor = q_factor[:, some].rearrange("p h j -> p (h j)").unsqueeze(2)
+                engine.tensor_tensor(out=rows, in0=rows, in1=factor.to_broadcast([P, at_once * J, D]), op=ALU.mult)
+                for h in range(h0, h0 + at_once):
                     store(out_0, rnd, h, q_res)
+
+        def scale_sums(engine_is_vector, q_sums, q_scaled, rnd, heads):
+            first = (rnd % 2) * HR
+            gains = inv_gain_sq[:, first + heads.start : first + heads.stop].unsqueeze(2).to_broadcast([P, len(heads), J])
+            mine = slice(heads.start, heads.stop)
+            if engine_is_vector:
+                nc.vector.scalar_tensor_tensor(
+                    out=q_scaled[:, mine], in0=q_sums[:, mine], scalar=EPS * EPS, in1=gains, op0=ALU.max, op1=ALU.mult
+                )
+            else:
+                nc.gpsimd.tensor_scalar(out=q_scaled[:, mine], in0=q_sums[:, mine], scalar1=EPS * EPS, scalar2=None, op0=ALU.max)
+                nc.gpsimd.tensor_tensor(out=q_scaled[:, mine], in0=q_scaled[:, mine], in1=gains, op=ALU.mult)
 
         table_warm = consts.tile([P, H], F32)
         nc.scalar.activation(out=table_warm[:], in_=ones[:, 0:H], func=ACT.Exp)
@@ -204,89 +250,188 @@ def tile_selfattention_pa_t_kernel(
         nc.gpsimd.tensor_scalar(
             out=inv_gain_sq[:], in0=inv_gain_sq_raw[:], scalar1=math.exp(-2.0 * MAX_LOG_GAIN), scalar2=None, op0=ALU.max
         )
+
+        def v_bank(rnd, v_res, i, acc=None):
+            add_bias(acc or project(V, rnd, i, psum_ring, "ring"), rnd, i, v_bias_sb, v_res)
+
+        def q_bank(rnd, q_res, i):
+            add_bias(project(Q, rnd, i, psum_ring, "ring"), rnd, i, q_bias_sb, q_res)
+
         grouped = regroup(transpose_words(0), (nc.vector.tensor_copy, nc.vector.tensor_copy))
+        v_bias_bank = spread(bias_rows[:, V_ROW, :])
         v_bias_sb = consts.tile([P, H, D], F32)
-        nc.scalar.copy(out=v_bias_sb[:].rearrange("p h d -> p (h d)"), in_=spread(bias_rows[:, V_ROW, :])[:])
-        grouped_1 = regroup(transpose_words(1), (nc.scalar.copy, nc.scalar.copy))
+        nc.scalar.copy(out=v_bias_sb[:].rearrange("p h d -> p (h d)"), in_=v_bias_bank[:])
         quantise(0, grouped)
-
-        def v_banks(rnd, v_res, some_banks):
-            for i in some_banks:
-                add_bias(project(V, rnd, i, psum_ring, "ring"), rnd, i, v_bias_sb, v_res)
-
-        v_res = results.tile([P, HR, J, D], F32, tag="v")
-        v_banks(0, v_res, range(0, BANKS // 2))
+        grouped = regroup(transpose_words(1), (nc.vector.tensor_copy, nc.scalar.copy))
         q_bias_sb = consts.tile([P, H, D], F32)
-        nc.scalar.copy(out=q_bias_sb[:].rearrange("p h d -> p (h d)"), in_=spread(bias_rows[:, Q_ROW, :])[:])
-        k_acc = [project(K, 0, i, psum_k, "k") for i in range(0, BANKS // 2)]
-        quantise(1, grouped_1)
-        v_banks(0, v_res, range(BANKS // 2, BANKS))
-        k_acc.extend([project(K, 0, i, psum_k, "k") for i in range(BANKS // 2, BANKS)])
-        banks = None
-        q_res = None
-        q_scaled = None
+        v_res = results.tile([P, HR, J, D], F32, tag="v")
+        q_res = results.tile([P, HR, J, D], F32, tag="q")
+        k_acc = [project(K, 0, 0, psum_k, "k")]
+        v_bank(0, v_res, 0)
+        k_acc.append(project(K, 0, 1, psum_k, "k"))
+        quantise(1, grouped)
+        v_bank(0, v_res, 1)
+        q_bias_bank = spread(bias_rows[:, Q_ROW, :])
+        k_sums = stage.tile([P, HR, J], F32, tag="k_sums")
+        k_squares = stage.tile([P, HR, J, D], BF16, tag="k_squares")
+        for i in range(0, BANKS // 2):
+            sum_squares(k_acc[i], k_squares, k_sums, i)
+        nc.scalar.copy(out=q_bias_sb[:].rearrange("p h d -> p (h d)"), in_=q_bias_bank[:])
+        for i in range(BANKS // 2, BANKS):
+            v_bank(0, v_res, i)
+            k_acc.append(project(K, 0, i, psum_k, "k"))
+        banks = transpose_words(2)
         q_factor = None
+        q_scaled = None
 
         for rnd in range(ROUNDS):
-            if rnd > 0:
+            last = rnd == ROUNDS - 1
+            if rnd > 0 or True:
                 if rnd + 2 < CHUNKS:
-                    grouped = regroup(banks, (nc.vector.tensor_copy, nc.scalar.copy))
+                    regrouped = new_grouped()
+                    regroup_bank(regrouped, 0, banks[0], nc.scalar.copy if rnd in S_BOTH else nc.vector.tensor_copy)
+                    if rnd > 0:
+                        regroup_bank(regrouped, 1, banks[1], nc.vector.tensor_copy if rnd in V_BOTH else nc.scalar.copy)
+            if rnd > 0 and not (last and 0):
                 v_res = results.tile([P, HR, J, D], F32, tag="v")
-                v_banks(rnd, v_res, range(BANKS))
-            for h in range(HR):
-                store(out_2, rnd, h, v_res)
+                for i in range(BANKS):
+                    v_bank(rnd, v_res, i, v_acc[i] if i < len(v_acc) else None)
+            if not (last and 0):
+                for h in range(HR):
+                    store(out_2, rnd, h, v_res)
 
-            k_sums = stage.tile([P, HR, J], F32, tag="k_sums")
-            k_squares = stage.tile([P, HR, J, D], BF16, tag="k_squares")
-            sum_squares(k_acc[0], k_squares, k_sums, 0)
             if rnd > 0:
-                q_factor = inverse_sqrt(q_scaled, "q_factor")
-            for i in range(1, BANKS):
+                k_sums = stage.tile([P, HR, J], F32, tag="k_sums")
+                k_squares = stage.tile([P, HR, J, D], BF16, tag="k_squares")
+                if rnd in K_RED:
+                    whole = stage.tile([P, PAIR, HR, D], F32, tag="whole", name="whole")
+                    nc.scalar.activation(out=whole[:], in_=k_acc[0][:], func=ACT.Square)
+                else:
+                    sum_squares(k_acc[0], k_squares, k_sums, 0)
+                if rnd not in K_RED:
+                    q_factor = inverse_sqrt(q_scaled, "q_factor")
+                sum_squares(k_acc[1], k_squares, k_sums, 1)
+                if rnd in K_RED:
+                    q_factor = inverse_sqrt(q_scaled, "q_factor")
+            for i in range(2, BANKS):
                 sum_squares(k_acc[i], k_squares, k_sums, i)
-            if rnd > 0:
-                scale_and_store_q(rnd - 1, q_res, q_factor, nc.gpsimd, HR // 2)
-
             if rnd == 0:
-                grouped = regroup(transpose_words(2), (nc.vector.tensor_copy, nc.scalar.copy))
-            q_res = results.tile([P, HR, J, D], F32, tag="q")
+                regroup_bank(regrouped, 1, banks[1], nc.vector.tensor_copy if rnd in V_BOTH else nc.scalar.copy)
+
+            q_before = q_res
+            if rnd > 0:
+                scale_and_store_q(rnd - 1, q_before, q_factor, nc.gpsimd, range(0, 2), 2)
+                if rnd in K_RED:
+                    nc.vector.tensor_reduce(
+                        out=like_bank(k_sums, 0).rearrange("p h j -> p j h"), in_=whole[:], axis=mybir.AxisListType.X, op=ALU.add
+                    )
+                q_res = results.tile([P, HR, J, D], F32, tag="q")
+            if rnd > 0 and Q_STORE_EARLY:
+                scale_and_store_q(rnd - 1, q_before, q_factor, nc.gpsimd, range(2, 4), 2)
             for i in range(BANKS):
-                add_bias(project(Q, rnd, i, psum_ring, "ring"), rnd, i, q_bias_sb, q_res)
+                q_bank(rnd, q_res, i)
+            if rnd == ROUNDS - 2 and 0:
+                v_res = results.tile([P, HR, J, D], F32, tag="v")
+                for i in range(0, 0):
+                    v_bank(rnd + 1, v_res, i)
+            fold = rnd in FOLD
+            g0 = GT if fold else 0
+            if fold and (not last or FOLD_EARLY):
+                folded = stage.tile([P, HR, GT, D], F32, tag="folded", name="folded")
+                fold_step(folded, q_res, D)
+                if last:
+                    fold_step(folded, q_res, D // 2)
+                    fold_step(folded, q_res, D // 4)
+            if rnd > 0 and not Q_STORE_EARLY:
+                scale_and_store_q(rnd - 1, q_before, q_factor, nc.gpsimd, range(2, 4), 2)
+            if not last and fold:
+                fold_step(folded, q_res, D // 2)
+            if not last and fold:
+                fold_step(folded, q_res, D // 4)
+            if last and fold and not FOLD_EARLY:
+                folded = stage.tile([P, HR, GT, D], F32, tag="folded", name="folded")
+                fold_step(folded, q_res, D)
+                fold_step(folded, q_res, D // 2)
+                fold_step(folded, q_res, D // 4)
             if rnd + 3 < CHUNKS:
                 banks = transpose_words(rnd + 3)
 
             q_sums = stage.tile([P, HR, J], F32, tag="q_sums")
             q_squares = stage.tile([P, HR, J, D], BF16, tag="q_squares")
-            sum_squares(like_bank(q_res, 0).rearrange("p h j d -> p j h d"), q_squares, q_sums, 0, range(0, 1))
-            k_over = excess(k_sums, "k_over")
-            sum_squares(like_bank(q_res, 0).rearrange("p h j d -> p j h d"), q_squares, q_sums, 0, range(1, PAIR))
-            k_factor = inverse_sqrt(k_over, "k_factor", bias=EPS * EPS)
-            for i in range(1, BANKS):
-                sum_squares(like_bank(q_res, i).rearrange("p h j d -> p j h d"), q_squares, q_sums, i)
-
+            q_scaled = stage.tile([P, HR, J], F32, tag="q_scaled")
             k_res = results.tile([P, HR, J, D], F32, tag="k")
-            for i in range(BANKS):
+
+            for i in range(BANKS - V_Q.get(rnd, 0), BANKS):
+                squares = stage.tile([P, HR, PAIR, D], F32, tag="v_squares", name="v_squares")
+                nc.vector.tensor_tensor(out=squares[:], in0=like_bank(q_res, i), in1=like_bank(q_res, i), op=ALU.mult)
+                nc.vector.tensor_reduce(out=like_bank(q_sums, i), in_=squares[:], axis=mybir.AxisListType.X, op=ALU.add)
+
+            def scale_k(i):
                 nc.vector.tensor_tensor(
                     out=like_bank(k_res, i).rearrange("p h j d -> p j h d"),
                     in0=k_acc[i][:],
                     in1=like_bank(k_factor, i).rearrange("p h j -> p j h").unsqueeze(3).to_broadcast([P, PAIR, HR, D]),
                     op=ALU.mult,
                 )
-                if rnd + 1 < ROUNDS:
-                    k_acc[i] = project(K, rnd + 1, i, psum_k, "k")
-                if i == BANKS // 2 - 1 and rnd + 2 < CHUNKS:
-                    quantise(rnd + 2, grouped)
-            for h in range(HR):
-                store(out_1, rnd, h, k_res)
 
-            heads = slice((rnd % 2) * HR, (rnd % 2 + 1) * HR)
-            q_scaled = stage.tile([P, HR, J], F32, tag="q_scaled")
-            nc.vector.scalar_tensor_tensor(
-                out=q_scaled[:],
-                in0=q_sums[:],
-                scalar=EPS * EPS,
-                in1=inv_gain_sq[:, heads].unsqueeze(2).to_broadcast([P, HR, J]),
-                op0=ALU.max,
-                op1=ALU.mult,
-            )
-
-        scale_and_store_q(ROUNDS - 1, q_res, inverse_sqrt(q_scaled, "q_factor"), nc.vector, 1)
+            if not last:
+                if EARLY == 2:
+                    k_over = excess(k_sums, "k_over")
+                q_tile(q_res, q_squares, q_sums, g0)
+                if EARLY == 0:
+                    k_over = excess(k_sums, "k_over")
+                    q_tile(q_res, q_squares, q_sums, g0 + 1)
+                if EARLY == 1:
+                    k_over = excess(k_sums, "k_over")
+                k_factor = inverse_sqrt(k_over, "k_factor", bias=EPS * EPS)
+                for j in range(g0 + 2 if EARLY == 0 else g0 + 1, J - PAIR * V_Q.get(rnd, 0)):
+                    q_tile(q_res, q_squares, q_sums, j)
+                for i in range(BANKS):
+                    scale_k(i)
+                    if i < BANKS // 2 or rnd + 2 >= CHUNKS:
+                        k_acc[i] = project(K, rnd + 1, i, psum_k, "k")
+                    if i == V_EARLY and not (rnd == ROUNDS - 2 and 0):
+                        v_acc = [project(V, rnd + 1, n, psum_ring, "ring") for n in range(BANKS // 2)]
+                if rnd + 2 < CHUNKS:
+                    quantise(rnd + 2, regrouped)
+                if V_EARLY is None:
+                    v_acc = [project(V, rnd + 1, i, psum_ring, "ring") for i in range(BANKS // 2)]
+                if rnd + 2 < CHUNKS:
+                    for i in range(BANKS // 2, BANKS):
+                        k_acc[i] = project(K, rnd + 1, i, psum_k, "k")
+                for h in range(HR):
+                    store(out_1, rnd, h, k_res)
+                if fold:
+                    sum_folded(folded, q_sums)
+                scale_sums(not G_SMALL, q_sums, q_scaled, rnd, range(HR))
+                if rnd == ROUNDS - 2 and 0:
+                    for i in range(0, BANKS):
+                        v_bank(rnd + 1, v_res, i)
+                    for h in range(HR):
+                        store(out_2, rnd + 1, h, v_res)
+            else:
+                q_tile(q_res, q_squares, q_sums, g0)
+                k_over = excess(k_sums, "k_over")
+                q_tile(q_res, q_squares, q_sums, g0 + 1)
+                k_factor = inverse_sqrt(k_over, "k_factor", bias=EPS * EPS)
+                for j in range(g0 + 2, J - PAIR * V_Q.get(rnd, 0)):
+                    q_tile(q_res, q_squares, q_sums, j)
+                for i in range(BANKS):
+                    if fold and i == RED_EARLY:
+                        sum_folded(folded, q_sums)
+                    scale_k(i)
+                    if HALF_K and i % 2 == 1:
+                        half = slice(4 * (i // 2), 4 * (i // 2) + 4)
+                        for h in range(HR):
+                            group, head = rnd // 2, (rnd % 2) * HR + h
+                            nc.sync.dma_start(
+                                out=out_1[E * group : E * group + E, head].rearrange("e (s j) d -> s e j d", j=J)[:, :, half],
+                                in_=k_res[:, h, half],
+                            )
+                if not HALF_K:
+                    for h in range(HR):
+                        store(out_1, rnd, h, k_res)
+                if fold and RED_EARLY is None:
+                    sum_folded(folded, q_sums)
+                scale_sums(True, q_sums, q_scaled, rnd, range(HR))
+                scale_and_store_q(rnd, q_res, inverse_sqrt(q_scaled, "q_factor"), nc.vector, range(HR))

@@ -21,26 +21,13 @@ E = 2
 J = E * L // P
 CHUNK = 4
 CHUNKS = B * L // (P * CHUNK)
-HR = 4
-ROUNDS = (B // E) * (H // HR)
 PAIR = 2
-BANKS = J // PAIR
+BANK = 512
+ROUNDS = [(g, h, 4) for g in range(4) for h in (0, 4)][:7] + [(3, 4, 2), (3, 6, 2)]
+LAST = len(ROUNDS) - 1
+FIRST_HALF = LAST - 1
 Q, K, V = 0, 1, 2
 V_ROW, Q_ROW = 0, 1
-GT = 1
-FOLD = ()
-S_BOTH = ()
-V_BOTH = ()
-V_Q = {}
-K_RED = ()
-G_SMALL = False
-EARLY = 0
-V_EARLY = 1
-Q_STORE_EARLY = True
-HALF_K = False
-RED_EARLY = 3
-FOLD_EARLY = True
-FOLDED = 16
 EPS = 1e-12
 MAX_LOG_GAIN = math.log(100.0)
 FLOPS = 2 * B * L * C * 3 * C
@@ -55,7 +42,7 @@ def tile_selfattention_pa_t_kernel(
         consts = ctx.enter_context(tc.tile_pool(name="consts", bufs=1))
         stage = ctx.enter_context(tc.tile_pool(name="stage", bufs=2))
         results = ctx.enter_context(tc.tile_pool(name="results", bufs=4))
-        psum_k = ctx.enter_context(tc.psum_pool(name="psum_k", bufs=BANKS))
+        psum_k = ctx.enter_context(tc.psum_pool(name="psum_k", bufs=4))
         psum_ring = ctx.enter_context(tc.psum_pool(name="psum_ring", bufs=4))
 
         x_sb = [consts.tile([P, CHUNK, C], BF16, name="x_sb%d" % c) for c in range(CHUNKS)]
@@ -70,7 +57,8 @@ def tile_selfattention_pa_t_kernel(
         gain_row = consts.tile([P, D], BF16)
         nc.vector.memset(gain_row[:].bitcast(I32), 0)
         nc.sync.dma_start(out=gain_row[0:1, 0:H], in_=log_scale_mul.rearrange("a h b c -> (a b c) h"))
-        load_x(0)
+        load_x(0, range(0, PAIR))
+        load_x(0, range(PAIR, CHUNK))
         load_x(1)
         ones = consts.tile([P, C], BF16)
         nc.vector.memset(ones[:], 1.0)
@@ -146,75 +134,65 @@ def tile_selfattention_pa_t_kernel(
                 in_=grouped[:, tiles.start : tiles.stop].rearrange("p j r t -> p (j r t)"),
             )
 
+        def heads_of(rnd):
+            group, first, count = ROUNDS[rnd]
+            return slice(first, first + count), count
+
+        def tiles_of_bank(rnd, i):
+            tiles = BANK // (ROUNDS[rnd][2] * D)
+            return range(tiles * i, tiles * (i + 1))
+
+        def banks_of(rnd):
+            return J * ROUNDS[rnd][2] * D // BANK
+
         def project(block, rnd, i, pool, tag):
-            group, first_column = rnd // 2, block * C + (rnd % 2) * HR * D
-            acc = pool.tile([P, PAIR, HR, D], F32, tag=tag)
-            for jj in range(PAIR):
-                tokens = slice((PAIR * i + jj) * P, (PAIR * i + jj + 1) * P)
+            group, first, count = ROUNDS[rnd]
+            first_column, width = block * C + first * D, count * D
+            tiles = tiles_of_bank(rnd, i)
+            acc = pool.tile([P, len(tiles), count, D], F32, tag=tag, name=tag)
+            for j in tiles:
+                tokens = slice(j * P, (j + 1) * P)
                 nc.tensor.matmul_mx(
-                    out=acc[:, jj].rearrange("p h d -> p (h d)"),
+                    out=acc[:, j - tiles.start].rearrange("p h d -> p (h d)"),
                     lhsT=x_codes[group][:, tokens].bitcast(FP8X4),
                     lhsT_scale=x_scales[group][:, tokens],
-                    rhs=w_words[:, 2 * first_column : 2 * (first_column + HR * D)].bitcast(FP4X4),
-                    rhs_scale=w_scales[:, first_column : first_column + HR * D],
+                    rhs=w_words[:, 2 * first_column : 2 * (first_column + width)].bitcast(FP4X4),
+                    rhs_scale=w_scales[:, first_column : first_column + width],
                     start=True,
                     stop=True,
                 )
             return acc
 
-        def like_bank(res, i):
-            return res[:, :, PAIR * i : PAIR * (i + 1)]
+        def like_bank(res, rnd, i):
+            tiles = tiles_of_bank(rnd, i)
+            return res[:, :, tiles.start : tiles.stop]
 
         def add_bias(acc, rnd, i, bias, res):
-            heads = slice((rnd % 2) * HR, (rnd % 2 + 1) * HR)
+            heads, count = heads_of(rnd)
             nc.vector.tensor_tensor(
-                out=like_bank(res, i).rearrange("p h j d -> p j h d"),
+                out=like_bank(res, rnd, i).rearrange("p h j d -> p j h d"),
                 in0=acc[:],
-                in1=bias[:, heads].unsqueeze(1).to_broadcast([P, PAIR, HR, D]),
+                in1=bias[:, heads].unsqueeze(1).to_broadcast([P, len(tiles_of_bank(rnd, i)), count, D]),
                 op=ALU.add,
             )
 
-        def sum_squares(rows_of_bank, squares, sums, i, tiles_of_bank=range(PAIR)):
-            for jj in tiles_of_bank:
-                j = PAIR * i + jj
-                for h in range(HR):
-                    nc.scalar.activation(
-                        out=squares[:, h, j, :],
-                        in_=rows_of_bank[:, jj, h, :],
-                        func=ACT.Square,
-                        accum_out=sums[:, h, j : j + 1],
-                    )
-
-        def q_tile(q_res, q_squares, q_sums, j):
-            sum_squares(
-                like_bank(q_res, j // PAIR).rearrange("p h j d -> p j h d"), q_squares, q_sums, j // PAIR, range(j % PAIR, j % PAIR + 1)
-            )
-
-        def fold_step(squares, q_res, width):
-            if width == D:
-                rows = q_res[:, :, 0:GT]
-                nc.gpsimd.tensor_tensor(out=squares[:], in0=rows, in1=rows, op=ALU.mult)
-            else:
-                low = squares[:, :, :, 0:width]
-                nc.gpsimd.tensor_tensor(out=low, in0=low, in1=squares[:, :, :, width : 2 * width], op=ALU.add)
-
-        def sum_folded(squares, sums):
-            nc.vector.tensor_reduce(out=sums[:, :, 0:GT], in_=squares[:, :, :, 0:FOLDED], axis=mybir.AxisListType.X, op=ALU.add)
+        def sum_row(row, squares, sums, h, j):
+            nc.scalar.activation(out=squares[:, h, j, :], in_=row, func=ACT.Square, accum_out=sums[:, h, j : j + 1])
 
         def store(dst, rnd, h, res):
-            group, head = rnd // 2, (rnd % 2) * HR + h
+            group, first, count = ROUNDS[rnd]
             nc.sync.dma_start(
-                out=dst[E * group : E * group + E, head].rearrange("e (s j) d -> s e (j d)", j=J),
+                out=dst[E * group : E * group + E, first + h].rearrange("e (s j) d -> s e (j d)", j=J),
                 in_=res[:, h].rearrange("p j d -> p (j d)"),
             )
 
-        def inverse_sqrt(values, tag, bias=0.0):
-            factor = stage.tile([P, HR, J], F32, tag=tag, name=tag)
+        def inverse_sqrt(values, tag, count, bias=0.0):
+            factor = stage.tile([P, count, J], F32, tag=tag, name=tag)
             nc.scalar.activation(out=factor[:], in_=values[:], func=ACT.Abs_reciprocal_sqrt, bias=bias)
             return factor
 
-        def excess(sums, tag):
-            over = stage.tile([P, HR, J], F32, tag=tag, name=tag)
+        def excess(sums, tag, count):
+            over = stage.tile([P, count, J], F32, tag=tag, name=tag)
             nc.scalar.activation(out=over[:], in_=sums[:], func=ACT.Relu, bias=-EPS * EPS)
             return over
 
@@ -227,35 +205,73 @@ def tile_selfattention_pa_t_kernel(
                 for h in range(h0, h0 + at_once):
                     store(out_0, rnd, h, q_res)
 
-        def scale_sums(engine_is_vector, q_sums, q_scaled, rnd, heads):
-            first = (rnd % 2) * HR
-            gains = inv_gain_sq[:, first + heads.start : first + heads.stop].unsqueeze(2).to_broadcast([P, len(heads), J])
-            mine = slice(heads.start, heads.stop)
-            if engine_is_vector:
-                nc.vector.scalar_tensor_tensor(
-                    out=q_scaled[:, mine], in0=q_sums[:, mine], scalar=EPS * EPS, in1=gains, op0=ALU.max, op1=ALU.mult
-                )
-            else:
-                nc.gpsimd.tensor_scalar(out=q_scaled[:, mine], in0=q_sums[:, mine], scalar1=EPS * EPS, scalar2=None, op0=ALU.max)
-                nc.gpsimd.tensor_tensor(out=q_scaled[:, mine], in0=q_scaled[:, mine], in1=gains, op=ALU.mult)
+        def scale_sums(rnd, q_sums):
+            heads, count = heads_of(rnd)
+            q_scaled = stage.tile([P, count, J], F32, tag="q_scaled", name="q_scaled")
+            nc.vector.scalar_tensor_tensor(
+                out=q_scaled[:],
+                in0=q_sums[:],
+                scalar=EPS * EPS,
+                in1=inv_gain_sq[:, heads].unsqueeze(2).to_broadcast([P, count, J]),
+                op0=ALU.max,
+                op1=ALU.mult,
+            )
+            return q_scaled
 
         table_warm = consts.tile([P, H], F32)
         nc.scalar.activation(out=table_warm[:], in_=ones[:, 0:H], func=ACT.Exp)
-        warm_up(3)
+        warm_up(2)
         inv_gain_sq_raw = consts.tile([P, H], F32)
         nc.scalar.activation(out=inv_gain_sq_raw[:], in_=spread(gain_row[:])[:, 0:H], func=ACT.Exp, scale=-2.0)
-        warm_up(2)
+        warm_up(1)
         nc.scalar.activation(out=table_warm[:], in_=inv_gain_sq_raw[:], func=ACT.Abs_reciprocal_sqrt)
         inv_gain_sq = consts.tile([P, H], F32)
         nc.gpsimd.tensor_scalar(
             out=inv_gain_sq[:], in0=inv_gain_sq_raw[:], scalar1=math.exp(-2.0 * MAX_LOG_GAIN), scalar2=None, op0=ALU.max
         )
 
-        def v_bank(rnd, v_res, i, acc=None):
-            add_bias(acc or project(V, rnd, i, psum_ring, "ring"), rnd, i, v_bias_sb, v_res)
+        def new_result(rnd, tag):
+            return results.tile([P, ROUNDS[rnd][2], J, D], F32, tag=tag, name=tag)
+
+        def new_sums(rnd, kind):
+            count = ROUNDS[rnd][2]
+            return (
+                stage.tile([P, count, J], F32, tag=kind + "_sums", name=kind + "_sums"),
+                stage.tile([P, count, J, D], BF16, tag=kind + "_squares", name=kind + "_squares"),
+            )
+
+        def v_bank(rnd, v_res, i):
+            add_bias(project(V, rnd, i, psum_ring, "ring"), rnd, i, v_bias_sb, v_res)
 
         def q_bank(rnd, q_res, i):
             add_bias(project(Q, rnd, i, psum_ring, "ring"), rnd, i, q_bias_sb, q_res)
+
+        def k_rows(rnd, i, acc, sums):
+            tiles = tiles_of_bank(rnd, i)
+            for j in tiles:
+                for h in range(ROUNDS[rnd][2]):
+                    sum_row(acc[:, j - tiles.start, h, :], sums[1], sums[0], h, j)
+
+        def q_rows(rnd, tiles, res, sums):
+            for j in tiles:
+                for h in range(ROUNDS[rnd][2]):
+                    sum_row(res[:, h, j, :], sums[1], sums[0], h, j)
+
+        def scale_k(rnd, i, acc, factor, res):
+            count = ROUNDS[rnd][2]
+            nc.vector.tensor_tensor(
+                out=like_bank(res, rnd, i).rearrange("p h j d -> p j h d"),
+                in0=acc[:],
+                in1=like_bank(factor, rnd, i)
+                .rearrange("p h j -> p j h")
+                .unsqueeze(3)
+                .to_broadcast([P, len(tiles_of_bank(rnd, i)), count, D]),
+                op=ALU.mult,
+            )
+
+        def store_all(dst, rnd, res):
+            for h in range(ROUNDS[rnd][2]):
+                store(dst, rnd, h, res)
 
         grouped = regroup(transpose_words(0), (nc.vector.tensor_copy, nc.vector.tensor_copy))
         v_bias_bank = spread(bias_rows[:, V_ROW, :])
@@ -263,175 +279,128 @@ def tile_selfattention_pa_t_kernel(
         nc.scalar.copy(out=v_bias_sb[:].rearrange("p h d -> p (h d)"), in_=v_bias_bank[:])
         quantise(0, grouped)
         grouped = regroup(transpose_words(1), (nc.vector.tensor_copy, nc.scalar.copy))
-        q_bias_sb = consts.tile([P, H, D], F32)
-        v_res = results.tile([P, HR, J, D], F32, tag="v")
-        q_res = results.tile([P, HR, J, D], F32, tag="q")
-        k_acc = [project(K, 0, 0, psum_k, "k")]
+        v_res = new_result(0, "v")
+        q_res = new_result(0, "q")
+        k_sums = new_sums(0, "k")
+        half = banks_of(0) // 2
         v_bank(0, v_res, 0)
-        k_acc.append(project(K, 0, 1, psum_k, "k"))
+        k_acc = [project(K, 0, i, psum_k, "k") for i in range(half)]
         quantise(1, grouped)
-        v_bank(0, v_res, 1)
+        for i in range(1, half):
+            v_bank(0, v_res, i)
         q_bias_bank = spread(bias_rows[:, Q_ROW, :])
-        k_sums = stage.tile([P, HR, J], F32, tag="k_sums")
-        k_squares = stage.tile([P, HR, J, D], BF16, tag="k_squares")
-        for i in range(0, BANKS // 2):
-            sum_squares(k_acc[i], k_squares, k_sums, i)
+        for i in range(half):
+            k_rows(0, i, k_acc[i], k_sums)
+        q_bias_sb = consts.tile([P, H, D], F32)
         nc.scalar.copy(out=q_bias_sb[:].rearrange("p h d -> p (h d)"), in_=q_bias_bank[:])
-        for i in range(BANKS // 2, BANKS):
+        for i in range(half, banks_of(0)):
             v_bank(0, v_res, i)
             k_acc.append(project(K, 0, i, psum_k, "k"))
-        banks = transpose_words(2)
-        q_factor = None
-        q_scaled = None
+            k_rows(0, i, k_acc[i], k_sums)
+        v_acc = []
 
-        for rnd in range(ROUNDS):
-            last = rnd == ROUNDS - 1
-            if rnd > 0 or True:
-                if rnd + 2 < CHUNKS:
-                    regrouped = new_grouped()
-                    regroup_bank(regrouped, 0, banks[0], nc.scalar.copy if rnd in S_BOTH else nc.vector.tensor_copy)
-                    if rnd > 0:
-                        regroup_bank(regrouped, 1, banks[1], nc.vector.tensor_copy if rnd in V_BOTH else nc.scalar.copy)
-            if rnd > 0 and not (last and 0):
-                v_res = results.tile([P, HR, J, D], F32, tag="v")
-                for i in range(BANKS):
-                    v_bank(rnd, v_res, i, v_acc[i] if i < len(v_acc) else None)
-            if not (last and 0):
-                for h in range(HR):
-                    store(out_2, rnd, h, v_res)
+        for rnd in range(FIRST_HALF):
+            banks_here, count = banks_of(rnd), ROUNDS[rnd][2]
+            new_x = rnd + 2 < CHUNKS
+            if rnd > 0:
+                if new_x:
+                    grouped = regroup(banks, (nc.vector.tensor_copy, nc.scalar.copy))
+                v_res = new_result(rnd, "v")
+                for i in range(banks_here):
+                    if i < len(v_acc):
+                        add_bias(v_acc[i], rnd, i, v_bias_sb, v_res)
+                    else:
+                        v_bank(rnd, v_res, i)
+            for h in range(count):
+                store(out_2, rnd, h, v_res)
 
             if rnd > 0:
-                k_sums = stage.tile([P, HR, J], F32, tag="k_sums")
-                k_squares = stage.tile([P, HR, J, D], BF16, tag="k_squares")
-                if rnd in K_RED:
-                    whole = stage.tile([P, PAIR, HR, D], F32, tag="whole", name="whole")
-                    nc.scalar.activation(out=whole[:], in_=k_acc[0][:], func=ACT.Square)
-                else:
-                    sum_squares(k_acc[0], k_squares, k_sums, 0)
-                if rnd not in K_RED:
-                    q_factor = inverse_sqrt(q_scaled, "q_factor")
-                sum_squares(k_acc[1], k_squares, k_sums, 1)
-                if rnd in K_RED:
-                    q_factor = inverse_sqrt(q_scaled, "q_factor")
-            for i in range(2, BANKS):
-                sum_squares(k_acc[i], k_squares, k_sums, i)
-            if rnd == 0:
-                regroup_bank(regrouped, 1, banks[1], nc.vector.tensor_copy if rnd in V_BOTH else nc.scalar.copy)
-
-            q_before = q_res
-            if rnd > 0:
-                scale_and_store_q(rnd - 1, q_before, q_factor, nc.gpsimd, range(0, 2), 2)
-                if rnd in K_RED:
-                    nc.vector.tensor_reduce(
-                        out=like_bank(k_sums, 0).rearrange("p h j -> p j h"), in_=whole[:], axis=mybir.AxisListType.X, op=ALU.add
-                    )
-                q_res = results.tile([P, HR, J, D], F32, tag="q")
-            if rnd > 0 and Q_STORE_EARLY:
-                scale_and_store_q(rnd - 1, q_before, q_factor, nc.gpsimd, range(2, 4), 2)
-            for i in range(BANKS):
+                k_sums = new_sums(rnd, "k")
+                k_rows(rnd, 0, k_acc[0], k_sums)
+                q_factor = inverse_sqrt(q_scaled, "q_factor", ROUNDS[rnd - 1][2])
+                for i in range(1, banks_here):
+                    k_rows(rnd, i, k_acc[i], k_sums)
+                scale_and_store_q(rnd - 1, q_res, q_factor, nc.gpsimd, range(ROUNDS[rnd - 1][2]), max(1, ROUNDS[rnd - 1][2] // 2))
+                q_res = new_result(rnd, "q")
+            for i in range(banks_here):
                 q_bank(rnd, q_res, i)
-            if rnd == ROUNDS - 2 and 0:
-                v_res = results.tile([P, HR, J, D], F32, tag="v")
-                for i in range(0, 0):
-                    v_bank(rnd + 1, v_res, i)
-            fold = rnd in FOLD
-            g0 = GT if fold else 0
-            if fold and (not last or FOLD_EARLY):
-                folded = stage.tile([P, HR, GT, D], F32, tag="folded", name="folded")
-                fold_step(folded, q_res, D)
-                if last:
-                    fold_step(folded, q_res, D // 2)
-                    fold_step(folded, q_res, D // 4)
-            if rnd > 0 and not Q_STORE_EARLY:
-                scale_and_store_q(rnd - 1, q_before, q_factor, nc.gpsimd, range(2, 4), 2)
-            if not last and fold:
-                fold_step(folded, q_res, D // 2)
-            if not last and fold:
-                fold_step(folded, q_res, D // 4)
-            if last and fold and not FOLD_EARLY:
-                folded = stage.tile([P, HR, GT, D], F32, tag="folded", name="folded")
-                fold_step(folded, q_res, D)
-                fold_step(folded, q_res, D // 2)
-                fold_step(folded, q_res, D // 4)
+            q_sums = new_sums(rnd, "q")
+            late_bank = None
+            if rnd == 0:
+                grouped = new_grouped()
+                banks = transpose_words(2)
+                regroup_bank(grouped, 0, banks[0], nc.vector.tensor_copy)
+                late_bank = banks[1]
+
+            step = 4 // count
+            q_rows(rnd, range(0, step), q_res, q_sums)
+            k_over = excess(k_sums[0], "k_over", count)
+            q_rows(rnd, range(step, 2 * step), q_res, q_sums)
+            k_factor = inverse_sqrt(k_over, "k_factor", count, bias=EPS * EPS)
+            if late_bank:
+                regroup_bank(grouped, 1, late_bank, nc.scalar.copy)
             if rnd + 3 < CHUNKS:
                 banks = transpose_words(rnd + 3)
+            q_rows(rnd, range(2 * step, J), q_res, q_sums)
 
-            q_sums = stage.tile([P, HR, J], F32, tag="q_sums")
-            q_squares = stage.tile([P, HR, J, D], BF16, tag="q_squares")
-            q_scaled = stage.tile([P, HR, J], F32, tag="q_scaled")
-            k_res = results.tile([P, HR, J, D], F32, tag="k")
+            k_res = new_result(rnd, "k")
+            k_next = []
+            for i in range(banks_here):
+                scale_k(rnd, i, k_acc[i], k_factor, k_res)
+                if rnd == FIRST_HALF - 1:
+                    k_next.append(project(K, FIRST_HALF + i // 2, i % 2, psum_k, "k"))
+                elif i < 2 or not new_x:
+                    k_next.append(project(K, rnd + 1, i, psum_k, "k"))
+                if i == 1:
+                    v_acc = [project(V, rnd + 1, n, psum_ring, "ring") for n in range(2)]
+            if new_x:
+                quantise(rnd + 2, grouped)
+                for i in range(2, banks_here):
+                    k_next.append(project(K, rnd + 1, i, psum_k, "k"))
+            for h in range(count):
+                store(out_1, rnd, h, k_res)
+            q_scaled = scale_sums(rnd, q_sums[0])
+            k_acc = k_next
 
-            for i in range(BANKS - V_Q.get(rnd, 0), BANKS):
-                squares = stage.tile([P, HR, PAIR, D], F32, tag="v_squares", name="v_squares")
-                nc.vector.tensor_tensor(out=squares[:], in0=like_bank(q_res, i), in1=like_bank(q_res, i), op=ALU.mult)
-                nc.vector.tensor_reduce(out=like_bank(q_sums, i), in_=squares[:], axis=mybir.AxisListType.X, op=ALU.add)
-
-            def scale_k(i):
-                nc.vector.tensor_tensor(
-                    out=like_bank(k_res, i).rearrange("p h j d -> p j h d"),
-                    in0=k_acc[i][:],
-                    in1=like_bank(k_factor, i).rearrange("p h j -> p j h").unsqueeze(3).to_broadcast([P, PAIR, HR, D]),
-                    op=ALU.mult,
-                )
-
-            if not last:
-                if EARLY == 2:
-                    k_over = excess(k_sums, "k_over")
-                q_tile(q_res, q_squares, q_sums, g0)
-                if EARLY == 0:
-                    k_over = excess(k_sums, "k_over")
-                    q_tile(q_res, q_squares, q_sums, g0 + 1)
-                if EARLY == 1:
-                    k_over = excess(k_sums, "k_over")
-                k_factor = inverse_sqrt(k_over, "k_factor", bias=EPS * EPS)
-                for j in range(g0 + 2 if EARLY == 0 else g0 + 1, J - PAIR * V_Q.get(rnd, 0)):
-                    q_tile(q_res, q_squares, q_sums, j)
-                for i in range(BANKS):
-                    scale_k(i)
-                    if i < BANKS // 2 or rnd + 2 >= CHUNKS:
-                        k_acc[i] = project(K, rnd + 1, i, psum_k, "k")
-                    if i == V_EARLY and not (rnd == ROUNDS - 2 and 0):
-                        v_acc = [project(V, rnd + 1, n, psum_ring, "ring") for n in range(BANKS // 2)]
-                if rnd + 2 < CHUNKS:
-                    quantise(rnd + 2, regrouped)
-                if V_EARLY is None:
-                    v_acc = [project(V, rnd + 1, i, psum_ring, "ring") for i in range(BANKS // 2)]
-                if rnd + 2 < CHUNKS:
-                    for i in range(BANKS // 2, BANKS):
-                        k_acc[i] = project(K, rnd + 1, i, psum_k, "k")
-                for h in range(HR):
-                    store(out_1, rnd, h, k_res)
-                if fold:
-                    sum_folded(folded, q_sums)
-                scale_sums(not G_SMALL, q_sums, q_scaled, rnd, range(HR))
-                if rnd == ROUNDS - 2 and 0:
-                    for i in range(0, BANKS):
-                        v_bank(rnd + 1, v_res, i)
-                    for h in range(HR):
-                        store(out_2, rnd + 1, h, v_res)
-            else:
-                q_tile(q_res, q_squares, q_sums, g0)
-                k_over = excess(k_sums, "k_over")
-                q_tile(q_res, q_squares, q_sums, g0 + 1)
-                k_factor = inverse_sqrt(k_over, "k_factor", bias=EPS * EPS)
-                for j in range(g0 + 2, J - PAIR * V_Q.get(rnd, 0)):
-                    q_tile(q_res, q_squares, q_sums, j)
-                for i in range(BANKS):
-                    if fold and i == RED_EARLY:
-                        sum_folded(folded, q_sums)
-                    scale_k(i)
-                    if HALF_K and i % 2 == 1:
-                        half = slice(4 * (i // 2), 4 * (i // 2) + 4)
-                        for h in range(HR):
-                            group, head = rnd // 2, (rnd % 2) * HR + h
-                            nc.sync.dma_start(
-                                out=out_1[E * group : E * group + E, head].rearrange("e (s j) d -> s e j d", j=J)[:, :, half],
-                                in_=k_res[:, h, half],
-                            )
-                if not HALF_K:
-                    for h in range(HR):
-                        store(out_1, rnd, h, k_res)
-                if fold and RED_EARLY is None:
-                    sum_folded(folded, q_sums)
-                scale_sums(True, q_sums, q_scaled, rnd, range(HR))
-                scale_and_store_q(rnd, q_res, inverse_sqrt(q_scaled, "q_factor"), nc.vector, range(HR))
+        a, b = FIRST_HALF, LAST
+        v_a, v_b = new_result(a, "v"), new_result(b, "v")
+        for i in range(2):
+            add_bias(v_acc[i], a, i, v_bias_sb, v_a)
+        store_all(out_2, a, v_a)
+        for i in range(2):
+            v_bank(b, v_b, i)
+        store_all(out_2, b, v_b)
+        sums_a, sums_b = new_sums(a, "k"), new_sums(b, "k")
+        k_rows(a, 0, k_acc[0], sums_a)
+        q_factor = inverse_sqrt(q_scaled, "q_factor", 4)
+        k_rows(a, 1, k_acc[1], sums_a)
+        scale_and_store_q(a - 1, q_res, q_factor, nc.gpsimd, range(4), 2)
+        q_a, q_b = new_result(a, "q"), new_result(b, "q")
+        for i in range(2):
+            q_bank(a, q_a, i)
+        for i in range(2):
+            q_bank(b, q_b, i)
+        k_rows(b, 0, k_acc[2], sums_b)
+        over_a = excess(sums_a[0], "k_over", 2)
+        k_rows(b, 1, k_acc[3], sums_b)
+        factor_a = inverse_sqrt(over_a, "k_factor", 2, bias=EPS * EPS)
+        q_sums_a, q_sums_b = new_sums(a, "q"), new_sums(b, "q")
+        q_rows(a, range(0, 2), q_a, q_sums_a)
+        over_b = excess(sums_b[0], "k_over", 2)
+        q_rows(a, range(2, 4), q_a, q_sums_a)
+        factor_b = inverse_sqrt(over_b, "k_factor", 2, bias=EPS * EPS)
+        q_rows(a, range(4, J), q_a, q_sums_a)
+        q_rows(b, range(0, 4), q_b, q_sums_b)
+        k_a, k_b = new_result(a, "k"), new_result(b, "k")
+        for i in range(2):
+            scale_k(a, i, k_acc[i], factor_a, k_a)
+        store_all(out_1, a, k_a)
+        scale_k(b, 0, k_acc[2], factor_b, k_b)
+        q_scaled_a = scale_sums(a, q_sums_a[0])
+        q_factor_a = inverse_sqrt(q_scaled_a, "q_factor", 2)
+        scale_k(b, 1, k_acc[3], factor_b, k_b)
+        store_all(out_1, b, k_b)
+        q_rows(b, range(4, J), q_b, q_sums_b)
+        scale_and_store_q(a, q_a, q_factor_a, nc.vector, range(2))
+        q_scaled_b = scale_sums(b, q_sums_b[0])
+        scale_and_store_q(b, q_b, inverse_sqrt(q_scaled_b, "q_factor", 2), nc.vector, range(2))

@@ -220,7 +220,7 @@ def tile_selfattention_pa_t_kernel(
 
         table_warm = consts.tile([P, H], F32)
         nc.scalar.activation(out=table_warm[:], in_=ones[:, 0:H], func=ACT.Exp)
-        warm_up(2)
+        warm_up(4)
         inv_gain_sq_raw = consts.tile([P, H], F32)
         nc.scalar.activation(out=inv_gain_sq_raw[:], in_=spread(gain_row[:])[:, 0:H], func=ACT.Exp, scale=-2.0)
         warm_up(1)
@@ -274,6 +274,7 @@ def tile_selfattention_pa_t_kernel(
                 store(dst, rnd, h, res)
 
         grouped = regroup(transpose_words(0), (nc.vector.tensor_copy, nc.vector.tensor_copy))
+        warm_up(1)
         v_bias_bank = spread(bias_rows[:, V_ROW, :])
         v_bias_sb = consts.tile([P, H, D], F32)
         nc.scalar.copy(out=v_bias_sb[:].rearrange("p h d -> p (h d)"), in_=v_bias_bank[:])

@@ -59,12 +59,13 @@ def tile_selfattention_pa_t_kernel(
         nc.sync.dma_start(out=gain_row[0:1, 0:H], in_=log_scale_mul.rearrange("a h b c -> (a b c) h"))
         load_x(0, range(0, PAIR))
         load_x(0, range(PAIR, CHUNK))
-        load_x(1)
         ones = consts.tile([P, C], BF16)
         nc.vector.memset(ones[:], 1.0)
         bias_rows = consts.tile([P, 2, C], BF16)
         nc.vector.memset(bias_rows[:].rearrange("p r c -> p (r c)").bitcast(I32), 0)
         nc.sync.dma_start(out=bias_rows[0:1, V_ROW, :], in_=v_bias.unsqueeze(0))
+        nc.sync.dma_start(out=bias_rows[0:1, Q_ROW, :], in_=q_bias.unsqueeze(0))
+        load_x(1)
         w_words = consts.tile([P, 2 * 3 * C], U8, align_bytes=64)
         nc.sync.dma_start(out=w_words[:].bitcast(I32), in_=W_qkv_words[0].bitcast(I32))
         w_scales = consts.tile([P, 3 * C], U8, align_bytes=64)
@@ -74,7 +75,6 @@ def tile_selfattention_pa_t_kernel(
                 out=w_scales[32 * quadrant : 32 * quadrant + 4, :].bitcast(I32),
                 in_=W_qkv_scales[0, 4 * quadrant : 4 * quadrant + 4, :].bitcast(I32),
             )
-        nc.sync.dma_start(out=bias_rows[0:1, Q_ROW, :], in_=q_bias.unsqueeze(0))
         for c in range(2, CHUNKS):
             load_x(c)
         identity = consts.tile([P, P], F32)
@@ -276,8 +276,11 @@ def tile_selfattention_pa_t_kernel(
         grouped = regroup(transpose_words(0), (nc.vector.tensor_copy, nc.vector.tensor_copy))
         warm_up(1)
         v_bias_bank = spread(bias_rows[:, V_ROW, :])
+        q_bias_bank = spread(bias_rows[:, Q_ROW, :])
         v_bias_sb = consts.tile([P, H, D], F32)
         nc.scalar.copy(out=v_bias_sb[:].rearrange("p h d -> p (h d)"), in_=v_bias_bank[:])
+        q_bias_sb = consts.tile([P, H, D], F32)
+        nc.scalar.copy(out=q_bias_sb[:].rearrange("p h d -> p (h d)"), in_=q_bias_bank[:])
         quantise(0, grouped)
         grouped = regroup(transpose_words(1), (nc.vector.tensor_copy, nc.scalar.copy))
         v_res = new_result(0, "v")
@@ -289,11 +292,8 @@ def tile_selfattention_pa_t_kernel(
         quantise(1, grouped)
         for i in range(1, half):
             v_bank(0, v_res, i)
-        q_bias_bank = spread(bias_rows[:, Q_ROW, :])
         for i in range(half):
             k_rows(0, i, k_acc[i], k_sums)
-        q_bias_sb = consts.tile([P, H, D], F32)
-        nc.scalar.copy(out=q_bias_sb[:].rearrange("p h d -> p (h d)"), in_=q_bias_bank[:])
         for i in range(half, banks_of(0)):
             v_bank(0, v_res, i)
             k_acc.append(project(K, 0, i, psum_k, "k"))

@@ -350,18 +350,33 @@ def tile_selfattention_pa_t_kernel(
                 scale_k(rnd, i, k_acc[i], k_factor, k_res)
                 if rnd == FIRST_HALF - 1:
                     k_next.append(project(K, FIRST_HALF + i // 2, i % 2, psum_k, "k"))
-                elif i < 2 or not new_x:
+                elif i < 2 or not new_x or rnd % 2 == 0:
                     k_next.append(project(K, rnd + 1, i, psum_k, "k"))
                 if i == 1:
                     v_acc = [project(V, rnd + 1, n, psum_ring, "ring") for n in range(2)]
             if new_x:
                 quantise(rnd + 2, grouped)
-                for i in range(2, banks_here):
+                for i in range(len(k_next), banks_here):
                     k_next.append(project(K, rnd + 1, i, psum_k, "k"))
             for h in range(count):
                 store(out_1, rnd, h, k_res)
             q_scaled = scale_sums(rnd, q_sums[0])
             k_acc = k_next
+
+        def head_rows(res, sums, h, tiles):
+            for j in tiles:
+                sum_row(res[:, h, j, :], sums[1], sums[0], h, j)
+
+        def scale_head(rnd, h, q_sums, q_scaled):
+            head = ROUNDS[rnd][1] + h
+            nc.vector.scalar_tensor_tensor(
+                out=q_scaled[:, h],
+                in0=q_sums[:, h],
+                scalar=EPS * EPS,
+                in1=inv_gain_sq[:, head : head + 1].to_broadcast([P, J]),
+                op0=ALU.max,
+                op1=ALU.mult,
+            )
 
         a, b = FIRST_HALF, LAST
         v_a, v_b = new_result(a, "v"), new_result(b, "v")
@@ -391,7 +406,7 @@ def tile_selfattention_pa_t_kernel(
         q_rows(a, range(2, 4), q_a, q_sums_a)
         factor_b = inverse_sqrt(over_b, "k_factor", 2, bias=EPS * EPS)
         q_rows(a, range(4, J), q_a, q_sums_a)
-        q_rows(b, range(0, 4), q_b, q_sums_b)
+        head_rows(q_b, q_sums_b, 0, range(J))
         k_a, k_b = new_result(a, "k"), new_result(b, "k")
         for i in range(2):
             scale_k(a, i, k_acc[i], factor_a, k_a)
@@ -401,7 +416,15 @@ def tile_selfattention_pa_t_kernel(
         q_factor_a = inverse_sqrt(q_scaled_a, "q_factor", 2)
         scale_k(b, 1, k_acc[3], factor_b, k_b)
         store_all(out_1, b, k_b)
-        q_rows(b, range(4, J), q_b, q_sums_b)
-        scale_and_store_q(a, q_a, q_factor_a, nc.vector, range(2))
-        q_scaled_b = scale_sums(b, q_sums_b[0])
-        scale_and_store_q(b, q_b, inverse_sqrt(q_scaled_b, "q_factor", 2), nc.vector, range(2))
+        head_rows(q_b, q_sums_b, 1, range(0, J // 2))
+        q_scaled_b = stage.tile([P, 2, J], F32, tag="q_scaled")
+        q_factor_b = stage.tile([P, 2, J], F32, tag="q_factor")
+        scale_and_store_q(a, q_a, q_factor_a, nc.vector, range(1))
+        scale_head(b, 0, q_sums_b[0], q_scaled_b)
+        nc.scalar.activation(out=q_factor_b[:, 0], in_=q_scaled_b[:, 0], func=ACT.Abs_reciprocal_sqrt)
+        scale_and_store_q(a, q_a, q_factor_a, nc.vector, range(1, 2))
+        head_rows(q_b, q_sums_b, 1, range(J // 2, J))
+        scale_and_store_q(b, q_b, q_factor_b, nc.vector, range(1))
+        scale_head(b, 1, q_sums_b[0], q_scaled_b)
+        nc.scalar.activation(out=q_factor_b[:, 1], in_=q_scaled_b[:, 1], func=ACT.Abs_reciprocal_sqrt)
+        scale_and_store_q(b, q_b, q_factor_b, nc.vector, range(1, 2))

import math
from contextlib import ExitStack

import concourse.mybir as mybir
from concourse.masks import make_identity

F32 = mybir.dt.float32
BF16 = mybir.dt.bfloat16
I32 = mybir.dt.int32
U32 = mybir.dt.uint32
U8 = mybir.dt.uint8
FP8X4 = mybir.dt.float8_e4m3fn_x4
FP4X4 = mybir.dt.float4_e2m1fn_x4
ALU = mybir.AluOpType
ACT = mybir.ActivationFunctionType

B, L, C, H, D = 8, 512, 512, 8, 64
P = 128
PACK = 4
E = 2
J = E * L // P
CHUNK = 4
CHUNKS = B * L // (P * CHUNK)
PAIR = 2
BANK = 512
ROUNDS = [(g, h, 4) for g in range(4) for h in (0, 4)][:7] + [(3, 4, 2), (3, 6, 2)]
LAST = len(ROUNDS) - 1
FIRST_HALF = LAST - 1
Q, K, V = 0, 1, 2
V_ROW, Q_ROW = 0, 1
EPS = 1e-12
MAX_LOG_GAIN = math.log(100.0)
FLOPS = 2 * B * L * C * 3 * C


def tile_selfattention_pa_t_kernel(
    tc, x, W_qkv_words, W_qkv_scales, q_bias, v_bias, log_scale_mul, out_0, out_1, out_2
):
    nc = tc.nc
    with ExitStack() as ctx:
        ctx.enter_context(tc.manual_schedule())
        consts = ctx.enter_context(tc.tile_pool(name="consts", bufs=1))
        stage = ctx.enter_context(tc.tile_pool(name="stage", bufs=2))
        results = ctx.enter_context(tc.tile_pool(name="results", bufs=4))
        psum_k = ctx.enter_context(tc.psum_pool(name="psum_k", bufs=4))
        psum_ring = ctx.enter_context(tc.psum_pool(name="psum_ring", bufs=4))

        x_sb = [consts.tile([P, CHUNK, C], BF16, name="x_sb%d" % c) for c in range(CHUNKS)]

        def load_x(c, tiles=range(CHUNK)):
            group, j0 = c // 2, CHUNK * (c % 2)
            tokens = x[E * group : E * group + E].rearrange("e (s j) c -> s e j c", j=J)
            nc.sync.dma_start(
                out=x_sb[c][:, tiles.start : tiles.stop, :], in_=tokens[:, :, j0 + tiles.start : j0 + tiles.stop, :]
            )

        gain_row = consts.tile([P, D], BF16)
        nc.vector.memset(gain_row[:].bitcast(I32), 0)
        nc.sync.dma_start(out=gain_row[0:1, 0:H], in_=log_scale_mul.rearrange("a h b c -> (a b c) h"))
        load_x(0, range(0, PAIR))
        load_x(0, range(PAIR, CHUNK))
        ones = consts.tile([P, C], BF16)
        nc.vector.memset(ones[:], 1.0)
        bias_rows = consts.tile([P, 2, C], BF16)
        nc.vector.memset(bias_rows[:].rearrange("p r c -> p (r c)").bitcast(I32), 0)
        nc.sync.dma_start(out=bias_rows[0:1, V_ROW, :], in_=v_bias.unsqueeze(0))
        nc.sync.dma_start(out=bias_rows[0:1, Q_ROW, :], in_=q_bias.unsqueeze(0))
        load_x(1)
        w_words = consts.tile([P, 2 * 3 * C], U8, align_bytes=64)
        nc.sync.dma_start(out=w_words[:].bitcast(I32), in_=W_qkv_words[0].bitcast(I32))
        w_scales = consts.tile([P, 3 * C], U8, align_bytes=64)
        nc.vector.memset(w_scales[:].bitcast(I32), 0)
        for quadrant in range(4):
            nc.sync.dma_start(
                out=w_scales[32 * quadrant : 32 * quadrant + 4, :].bitcast(I32),
                in_=W_qkv_scales[0, 4 * quadrant : 4 * quadrant + 4, :].bitcast(I32),
            )
        for c in range(2, CHUNKS):
            load_x(c)
        identity = consts.tile([P, P], F32)
        make_identity(nc, identity[:])

        def spread(row):
            bank = psum_ring.tile([P, C], F32, tag="ring")
            nc.tensor.matmul(out=bank[:, 0 : row.shape[1]], lhsT=ones[:, 0:P], rhs=row, start=True, stop=True)
            return bank

        def warm_up(passes):
            for i in range(passes):
                bank = psum_ring.tile([P, C], F32, tag="ring", name="warm")
                nc.tensor.matmul(out=bank[:], lhsT=ones[:, 0:P], rhs=ones[:], start=True, stop=True)

        def transpose_bank(c, i):
            bank = psum_ring.tile([P, PAIR, 2, P], F32, tag="ring")
            for jj in range(PAIR):
                words = x_sb[c][:, PAIR * i + jj, :].bitcast(F32)
                for u in range(2):
                    nc.tensor.transpose(bank[:, jj, u, :], words[:, u : C // 2 : 2], identity[:])
            return bank

        def transpose_words(c):
            return [transpose_bank(c, i) for i in range(CHUNK // PAIR)]

        def new_grouped():
            return stage.tile([P, CHUNK, P, PACK], BF16, align_bytes=64, tag="grouped", name="grouped")

        def regroup_bank(grouped, i, bank, copy):
            copy(
                out=grouped[:, PAIR * i : PAIR * (i + 1)]
                .rearrange("p j r t -> p (j r t)")
                .bitcast(F32)
                .rearrange("p (j r u) -> p j r u", j=PAIR, u=2),
                in_=bank[:].rearrange("p j u r -> p j r u"),
            )

        def regroup(banks, copies):
            grouped = new_grouped()
            for i in range(CHUNK // PAIR):
                regroup_bank(grouped, i, banks[i], copies[i])
            return grouped

        x_codes = {}
        x_scales = {}

        def quantise(c, grouped, tiles=range(CHUNK)):
            group, j0 = c // 2, CHUNK * (c % 2)
            if j0 == 0 and tiles.start == 0:
                x_codes[group] = stage.tile([P, J * P], U32, align_bytes=64, tag="codes", name="codes")
                x_scales[group] = stage.tile([P, J * P], U8, align_bytes=64, tag="scales", name="scales")
            columns = slice((j0 + tiles.start) * P, (j0 + tiles.stop) * P)
            nc.vector.quantize_mx(
                out=x_codes[group][:, columns].bitcast(FP8X4),
                scales=x_scales[group][:, columns],
                in_=grouped[:, tiles.start : tiles.stop].rearrange("p j r t -> p (j r t)"),
            )

        def heads_of(rnd):
            group, first, count = ROUNDS[rnd]
            return slice(first, first + count), count

        def tiles_of_bank(rnd, i):
            tiles = BANK // (ROUNDS[rnd][2] * D)
            return range(tiles * i, tiles * (i + 1))

        def banks_of(rnd):
            return J * ROUNDS[rnd][2] * D // BANK

        def project(block, rnd, i, pool, tag):
            group, first, count = ROUNDS[rnd]
            first_column, width = block * C + first * D, count * D
            tiles = tiles_of_bank(rnd, i)
            acc = pool.tile([P, len(tiles), count, D], F32, tag=tag, name=tag)
            for j in tiles:
                tokens = slice(j * P, (j + 1) * P)
                nc.tensor.matmul_mx(
                    out=acc[:, j - tiles.start].rearrange("p h d -> p (h d)"),
                    lhsT=x_codes[group][:, tokens].bitcast(FP8X4),
                    lhsT_scale=x_scales[group][:, tokens],
                    rhs=w_words[:, 2 * first_column : 2 * (first_column + width)].bitcast(FP4X4),
                    rhs_scale=w_scales[:, first_column : first_column + width],
                    start=True,
                    stop=True,
                )
            return acc

        def like_bank(res, rnd, i):
            tiles = tiles_of_bank(rnd, i)
            return res[:, :, tiles.start : tiles.stop]

        def add_bias(acc, rnd, i, bias, res):
            heads, count = heads_of(rnd)
            nc.vector.tensor_tensor(
                out=like_bank(res, rnd, i).rearrange("p h j d -> p j h d"),
                in0=acc[:],
                in1=bias[:, heads].unsqueeze(1).to_broadcast([P, len(tiles_of_bank(rnd, i)), count, D]),
                op=ALU.add,
            )

        def sum_row(row, squares, sums, h, j):
            nc.scalar.activation(out=squares[:, h, j, :], in_=row, func=ACT.Square, accum_out=sums[:, h, j : j + 1])

        def store(dst, rnd, h, res):
            group, first, count = ROUNDS[rnd]
            nc.sync.dma_start(
                out=dst[E * group : E * group + E, first + h].rearrange("e (s j) d -> s e (j d)", j=J),
                in_=res[:, h].rearrange("p j d -> p (j d)"),
            )

        def inverse_sqrt(values, tag, count, bias=0.0):
            factor = stage.tile([P, count, J], F32, tag=tag, name=tag)
            nc.scalar.activation(out=factor[:], in_=values[:], func=ACT.Abs_reciprocal_sqrt, bias=bias)
            return factor

        def excess(sums, tag, count):
            over = stage.tile([P, count, J], F32, tag=tag, name=tag)
            nc.scalar.activation(out=over[:], in_=sums[:], func=ACT.Relu, bias=-EPS * EPS)
            return over

        def scale_and_store_q(rnd, q_res, q_factor, engine, heads, at_once=1):
            for h0 in heads[::at_once]:
                some = slice(h0, h0 + at_once)
                rows = q_res[:, some].rearrange("p h j d -> p (h j) d")
                factor = q_factor[:, some].rearrange("p h j -> p (h j)").unsqueeze(2)
                engine.tensor_tensor(out=rows, in0=rows, in1=factor.to_broadcast([P, at_once * J, D]), op=ALU.mult)
                for h in range(h0, h0 + at_once):
                    store(out_0, rnd, h, q_res)

        def scale_sums(rnd, q_sums):
            heads, count = heads_of(rnd)
            q_scaled = stage.tile([P, count, J], F32, tag="q_scaled", name="q_scaled")
            nc.vector.scalar_tensor_tensor(
                out=q_scaled[:],
                in0=q_sums[:],
                scalar=EPS * EPS,
                in1=inv_gain_sq[:, heads].unsqueeze(2).to_broadcast([P, count, J]),
                op0=ALU.max,
                op1=ALU.mult,
            )
            return q_scaled

        table_warm = consts.tile([P, H], F32)
        nc.scalar.activation(out=table_warm[:], in_=ones[:, 0:H], func=ACT.Exp)
        warm_up(4)
        inv_gain_sq_raw = consts.tile([P, H], F32)
        nc.scalar.activation(out=inv_gain_sq_raw[:], in_=spread(gain_row[:])[:, 0:H], func=ACT.Exp, scale=-2.0)
        warm_up(1)
        nc.scalar.activation(out=table_warm[:], in_=inv_gain_sq_raw[:], func=ACT.Abs_reciprocal_sqrt)
        inv_gain_sq = consts.tile([P, H], F32)
        nc.gpsimd.tensor_scalar(
            out=inv_gain_sq[:], in0=inv_gain_sq_raw[:], scalar1=math.exp(-2.0 * MAX_LOG_GAIN), scalar2=None, op0=ALU.max
        )

        def new_result(rnd, tag):
            return results.tile([P, ROUNDS[rnd][2], J, D], F32, tag=tag, name=tag)

        def new_sums(rnd, kind):
            count = ROUNDS[rnd][2]
            return (
                stage.tile([P, count, J], F32, tag=kind + "_sums", name=kind + "_sums"),
                stage.tile([P, count, J, D], BF16, tag=kind + "_squares", name=kind + "_squares"),
            )

        def v_bank(rnd, v_res, i):
            add_bias(project(V, rnd, i, psum_ring, "ring"), rnd, i, v_bias_sb, v_res)

        def q_bank(rnd, q_res, i):
            add_bias(project(Q, rnd, i, psum_ring, "ring"), rnd, i, q_bias_sb, q_res)

        def k_rows(rnd, i, acc, sums):
            tiles = tiles_of_bank(rnd, i)
            for j in tiles:
                for h in range(ROUNDS[rnd][2]):
                    sum_row(acc[:, j - tiles.start, h, :], sums[1], sums[0], h, j)

        def q_rows(rnd, tiles, res, sums):
            for j in tiles:
                for h in range(ROUNDS[rnd][2]):
                    sum_row(res[:, h, j, :], sums[1], sums[0], h, j)

        def scale_k(rnd, i, acc, factor, res):
            count = ROUNDS[rnd][2]
            nc.vector.tensor_tensor(
                out=like_bank(res, rnd, i).rearrange("p h j d -> p j h d"),
                in0=acc[:],
                in1=like_bank(factor, rnd, i)
                .rearrange("p h j -> p j h")
                .unsqueeze(3)
                .to_broadcast([P, len(tiles_of_bank(rnd, i)), count, D]),
                op=ALU.mult,
            )

        def store_all(dst, rnd, res):
            for h in range(ROUNDS[rnd][2]):
                store(dst, rnd, h, res)

        grouped = regroup(transpose_words(0), (nc.vector.tensor_copy, nc.vector.tensor_copy))
        warm_up(1)
        v_bias_bank = spread(bias_rows[:, V_ROW, :])
        q_bias_bank = spread(bias_rows[:, Q_ROW, :])
        v_bias_sb = consts.tile([P, H, D], F32)
        nc.scalar.copy(out=v_bias_sb[:].rearrange("p h d -> p (h d)"), in_=v_bias_bank[:])
        q_bias_sb = consts.tile([P, H, D], F32)
        nc.scalar.copy(out=q_bias_sb[:].rearrange("p h d -> p (h d)"), in_=q_bias_bank[:])
        quantise(0, grouped)
        grouped = regroup(transpose_words(1), (nc.vector.tensor_copy, nc.scalar.copy))
        v_res = new_result(0, "v")
        q_res = new_result(0, "q")
        k_sums = new_sums(0, "k")
        half = banks_of(0) // 2
        v_bank(0, v_res, 0)
        k_acc = [project(K, 0, i, psum_k, "k") for i in range(half)]
        quantise(1, grouped)
        for i in range(1, half):
            v_bank(0, v_res, i)
        for i in range(half):
            k_rows(0, i, k_acc[i], k_sums)
        for i in range(half, banks_of(0)):
            v_bank(0, v_res, i)
            k_acc.append(project(K, 0, i, psum_k, "k"))
            k_rows(0, i, k_acc[i], k_sums)
        v_acc = []

        for rnd in range(FIRST_HALF):
            banks_here, count = banks_of(rnd), ROUNDS[rnd][2]
            new_x = rnd + 2 < CHUNKS
            if rnd > 0:
                if new_x:
                    grouped = regroup(banks, (nc.vector.tensor_copy, nc.scalar.copy))
                v_res = new_result(rnd, "v")
                for i in range(banks_here):
                    if i < len(v_acc):
                        add_bias(v_acc[i], rnd, i, v_bias_sb, v_res)
                    else:
                        v_bank(rnd, v_res, i)
            for h in range(count):
                store(out_2, rnd, h, v_res)

            if rnd > 0:
                k_sums = new_sums(rnd, "k")
                k_rows(rnd, 0, k_acc[0], k_sums)
                q_factor = inverse_sqrt(q_scaled, "q_factor", ROUNDS[rnd - 1][2])
                for i in range(1, banks_here):
                    k_rows(rnd, i, k_acc[i], k_sums)
                scale_and_store_q(rnd - 1, q_res, q_factor, nc.gpsimd, range(ROUNDS[rnd - 1][2]), max(1, ROUNDS[rnd - 1][2] // 2))
                q_res = new_result(rnd, "q")
            for i in range(banks_here):
                q_bank(rnd, q_res, i)
            q_sums = new_sums(rnd, "q")
            late_bank = None
            if rnd == 0:
                grouped = new_grouped()
                banks = transpose_words(2)
                regroup_bank(grouped, 0, banks[0], nc.vector.tensor_copy)
                late_bank = banks[1]

            step = 4 // count
            q_rows(rnd, range(0, step), q_res, q_sums)
            k_over = excess(k_sums[0], "k_over", count)
            q_rows(rnd, range(step, 2 * step), q_res, q_sums)
            k_factor = inverse_sqrt(k_over, "k_factor", count, bias=EPS * EPS)
            if late_bank:
                regroup_bank(grouped, 1, late_bank, nc.scalar.copy)
            if rnd + 3 < CHUNKS:
                banks = transpose_words(rnd + 3)
            q_rows(rnd, range(2 * step, J), q_res, q_sums)

            k_res = new_result(rnd, "k")
            k_next = []
            for i in range(banks_here):
                scale_k(rnd, i, k_acc[i], k_factor, k_res)
                if rnd == FIRST_HALF - 1:
                    k_next.append(project(K, FIRST_HALF + i // 2, i % 2, psum_k, "k"))
                elif i < 2 or not new_x or rnd % 2 == 0:
                    k_next.append(project(K, rnd + 1, i, psum_k, "k"))
                if i == 1:
                    v_acc = [project(V, rnd + 1, n, psum_ring, "ring") for n in range(2)]
            if new_x:
                quantise(rnd + 2, grouped)
                for i in range(len(k_next), banks_here):
                    k_next.append(project(K, rnd + 1, i, psum_k, "k"))
            for h in range(count):
                store(out_1, rnd, h, k_res)
            q_scaled = scale_sums(rnd, q_sums[0])
            k_acc = k_next

        def head_rows(res, sums, h, tiles):
            for j in tiles:
                sum_row(res[:, h, j, :], sums[1], sums[0], h, j)

        def scale_head(rnd, h, q_sums, q_scaled):
            head = ROUNDS[rnd][1] + h
            nc.vector.scalar_tensor_tensor(
                out=q_scaled[:, h],
                in0=q_sums[:, h],
                scalar=EPS * EPS,
                in1=inv_gain_sq[:, head : head + 1].to_broadcast([P, J]),
                op0=ALU.max,
                op1=ALU.mult,
            )

        a, b = FIRST_HALF, LAST
        v_a, v_b = new_result(a, "v"), new_result(b, "v")
        for i in range(2):
            add_bias(v_acc[i], a, i, v_bias_sb, v_a)
        store_all(out_2, a, v_a)
        for i in range(2):
            v_bank(b, v_b, i)
        store_all(out_2, b, v_b)
        sums_a, sums_b = new_sums(a, "k"), new_sums(b, "k")
        k_rows(a, 0, k_acc[0], sums_a)
        q_factor = inverse_sqrt(q_scaled, "q_factor", 4)
        k_rows(a, 1, k_acc[1], sums_a)
        scale_and_store_q(a - 1, q_res, q_factor, nc.gpsimd, range(4), 2)
        q_a, q_b = new_result(a, "q"), new_result(b, "q")
        for i in range(2):
            q_bank(a, q_a, i)
        for i in range(2):
            q_bank(b, q_b, i)
        k_rows(b, 0, k_acc[2], sums_b)
        over_a = excess(sums_a[0], "k_over", 2)
        k_rows(b, 1, k_acc[3], sums_b)
        factor_a = inverse_sqrt(over_a, "k_factor", 2, bias=EPS * EPS)
        q_sums_a, q_sums_b = new_sums(a, "q"), new_sums(b, "q")
        q_rows(a, range(0, 2), q_a, q_sums_a)
        over_b = excess(sums_b[0], "k_over", 2)
        q_rows(a, range(2, 4), q_a, q_sums_a)
        factor_b = inverse_sqrt(over_b, "k_factor", 2, bias=EPS * EPS)
        q_rows(a, range(4, J), q_a, q_sums_a)
        head_rows(q_b, q_sums_b, 0, range(J))
        k_a, k_b = new_result(a, "k"), new_result(b, "k")
        for i in range(2):
            scale_k(a, i, k_acc[i], factor_a, k_a)
        store_all(out_1, a, k_a)
        scale_k(b, 0, k_acc[2], factor_b, k_b)
        q_scaled_a = scale_sums(a, q_sums_a[0])
        q_factor_a = inverse_sqrt(q_scaled_a, "q_factor", 2)
        scale_k(b, 1, k_acc[3], factor_b, k_b)
        store_all(out_1, b, k_b)
        head_rows(q_b, q_sums_b, 1, range(0, J // 2))
        q_scaled_b = stage.tile([P, 2, J], F32, tag="q_scaled")
        q_factor_b = stage.tile([P, 2, J], F32, tag="q_factor")
        scale_and_store_q(a, q_a, q_factor_a, nc.vector, range(1))
        scale_head(b, 0, q_sums_b[0], q_scaled_b)
        nc.scalar.activation(out=q_factor_b[:, 0], in_=q_scaled_b[:, 0], func=ACT.Abs_reciprocal_sqrt)
        scale_and_store_q(a, q_a, q_factor_a, nc.vector, range(1, 2))
        head_rows(q_b, q_sums_b, 1, range(J // 2, J))
        scale_and_store_q(b, q_b, q_factor_b, nc.vector, range(1))
        scale_head(b, 1, q_sums_b[0], q_scaled_b)
        nc.scalar.activation(out=q_factor_b[:, 1], in_=q_scaled_b[:, 1], func=ACT.Abs_reciprocal_sqrt)
        scale_and_store_q(b, q_b, q_factor_b, nc.vector, range(1, 2))
